import numpy as np
import ml_dtypes


def mxq(x, axis, fmt="e4m3"):
    dtype, down = {"e4m3": (ml_dtypes.float8_e4m3fn, 7), "e5m2": (ml_dtypes.float8_e5m2, 14)}[fmt]
    v = np.moveaxis(np.asarray(x, np.float32).astype(ml_dtypes.bfloat16).astype(np.float64), axis, -1)
    blocks = v.reshape(v.shape[:-1] + (-1, 32))
    amax = np.abs(blocks).max(-1, keepdims=True)
    byte = np.maximum(np.where(amax > 0, np.frexp(amax)[1] - 1 + 127, 0) - down, 1)
    scale = np.exp2(byte - 127.0)
    codes = (blocks / scale).astype(np.float32).astype(dtype).astype(np.float64)
    return np.moveaxis((codes * scale).reshape(v.shape), -1, axis)


WIDE = False


def mx_kscale(k):
    if not WIDE:
        return np.ones(k)
    levels = np.array([10, -10, 5, -5, 0])
    if k % 512:
        return np.exp2(np.random.permutation(np.resize(levels, k // 32))).repeat(32)
    a = np.empty((k // 512, 16))
    for p in range(k // 512):
        a[p, :8] = np.random.permutation(np.resize(levels, 8))
        for g in range(8):
            far = levels[np.abs(levels - a[p, g]) >= 10]
            a[p, g + 8] = far[np.random.randint(len(far))]
    return np.exp2(a.ravel()).repeat(32)


BF16 = ml_dtypes.bfloat16


def bf(x):
    return np.asarray(x, np.float32).astype(BF16)


def f64(x):
    return np.asarray(x).astype(np.float64)


B, T, HS, WS, G, K, CB, CB2, CB3, CB4 = 4, 64, 4, 4, 2, 1024, 128, 160, 200, 250
EPS = 1e-3
NV = 5
R = B * T * HS * WS


def bn_apply(v, p):
    gamma, beta, mean, var = p[0], p[1], p[2], p[3]
    return (v - mean) * (gamma / np.sqrt(var + EPS)) + beta


def dwconv_t(v, taps, d):
    vp = np.pad(v, ((0, 0), (d, d), (0, 0), (0, 0), (0, 0), (0, 0)))
    return taps[0] * vp[:, 0:T] + taps[1] * vp[:, d:d + T] + taps[2] * vp[:, 2 * d:2 * d + T]


def setup_inputs():
    s = mx_kscale(K)
    gamma = 1.0 + 0.1 * np.random.standard_normal((NV, G, CB))
    beta = 0.2 * np.random.standard_normal((NV, G, CB))
    mean = 0.04 * np.random.standard_normal((NV, G, CB))
    var = np.random.uniform(0.01, 0.04, (NV, G, CB))
    return {"x": bf(np.random.standard_normal((B, T, HS, WS, G * K)) * np.tile(s, G)),
            "w": bf(np.random.standard_normal((NV, G, K, CB)) * 0.15 / np.sqrt(K) / s[:, None]),
            "b": bf(np.random.standard_normal((NV, G, CB)) * 0.04),
            "dw": bf(np.random.standard_normal((3, 3, G, CB)) * 0.6),
            "bn": bf(np.stack([gamma, beta, mean, var], axis=1))}


def reference(x, w, b, dw, bn):
    b, dw, bn = f64(b), f64(dw), f64(bn)
    xg = f64(x).reshape(R, G, K).transpose(1, 0, 2)
    wg = f64(w).transpose(1, 2, 0, 3).reshape(G, K, NV * CB)
    y = mxq(xg, 2, "e4m3") @ mxq(wg, 1, "e4m3")
    y = y.reshape(G, B, T, HS, WS, NV, CB).transpose(5, 1, 2, 3, 4, 0, 6) + b[:, None, None, None, None]
    outs = [bn_apply(y[0], bn[0])]
    for i, d in enumerate((1, 2, 3)):
        outs.append(bn_apply(dwconv_t(y[1 + i], dw[i], d), bn[1 + i]))
    t5 = np.maximum(y[4], np.concatenate([y[4][:, 1:], y[4][:, -1:]], axis=1))
    outs.append(bn_apply(t5, bn[4]))
    z = np.stack(outs, axis=5)
    z = np.maximum(z.reshape(B, T, HS, WS, G * NV * CB), 0.0)
    z = z.reshape(B, T, HS, WS, G, NV * CB).swapaxes(-1, -2).reshape(B, T, HS, WS, G * NV * CB)
    return z.reshape(B, T // 2, 2, HS, WS, G * NV * CB).max(axis=2)

@@ -1,0 +1,449 @@
+from contextlib import ExitStack
+
+import concourse.mybir as mybir
+from concourse.masks import make_identity
+
+F32 = mybir.dt.float32
+BF16 = mybir.dt.bfloat16
+U32 = mybir.dt.uint32
+U8 = mybir.dt.uint8
+FP8X4 = mybir.dt.float8_e4m3fn_x4
+ALU = mybir.AluOpType
+ACT = mybir.ActivationFunctionType
+
+P = 128
+B, T, HW, G, K, CB, NV = 4, 64, 16, 2, 1024, 128, 5
+EPS = 1e-3
+FLOPS = 2 * B * T * HW * G * K * NV * CB
+
+TC = 16
+NCH = T // TC
+SEG = TC * HW
+NH = TC // 2
+NSTEP = (B // 2) * NCH
+PASS_COLS = 2 * SEG
+OUT_V = G * CB
+
+ORDER = (4, 3, 2, 1, 0)
+NU = NSTEP * NV
+X_AHEAD = (0, 0, 2, 3, 3, 3, 3, 3)
+POOL_LAG = {0: 1, 1: 1, 2: 1, 3: 1, 4: 2}
+BACK_LAG = 2
+STORE_BY_BRANCH_FROM = NSTEP - 2
+ROW_DW = NV * G
+ROW_BN = ROW_DW + 3 * 3 * G
+N_PARAM_ROWS = ROW_BN + NV * 4 * G
+PASS_WORDS = 256
+
+
+def tile_timeception_pa_t_kernel(tc, x, w, b, dw, bn, out):
+    nc = tc.nc
+    with ExitStack() as ctx:
+        ctx.enter_context(tc.manual_schedule())
+        const = ctx.enter_context(tc.tile_pool(name="const", bufs=1))
+        keep = ctx.enter_context(tc.tile_pool(name="keep", bufs=1))
+        x_in = ctx.enter_context(tc.tile_pool(name="x_in", bufs=2))
+        x_grouped = ctx.enter_context(tc.tile_pool(name="x_grouped", bufs=2))
+        x_mx = ctx.enter_context(tc.tile_pool(name="x_mx", bufs=4))
+        normed0 = ctx.enter_context(tc.tile_pool(name="normed0", bufs=3))
+        out_small = ctx.enter_context(tc.tile_pool(name="out_small", bufs=2 * NV))
+        pooled_pool = ctx.enter_context(tc.tile_pool(name="pooled_pool", bufs=2))
+        out_pool = ctx.enter_context(tc.tile_pool(name="out_pool", bufs=2))
+        ps_x = ctx.enter_context(tc.psum_pool(name="ps_x", bufs=2))
+        ps_y = ctx.enter_context(tc.psum_pool(name="ps_y", bufs=4))
+        ps_back = ctx.enter_context(tc.psum_pool(name="ps_back", bufs=2))
+
+        x_raw = {}
+
+        def load_x(s):
+            pair, tcn = divmod(s, NCH)
+            raw = x_in.tile([P, 4, G * K], BF16, name="raw")
+            for nl in range(2):
+                src = x[2 * pair + nl, tcn * TC:(tcn + 1) * TC]
+                nc.sync.dma_start(
+                    out=raw[:, 2 * nl:2 * nl + 2, :],
+                    in_=src.rearrange("(h t) p q c -> (t p q) h c", h=2),
+                )
+            x_raw[s] = raw
+
+        w_stage = {}
+
+        def load_w(n):
+            pool, tag = (pooled_pool, "pooled") if n % 2 == 0 else (out_pool, "out_rows")
+            stage = pool.tile([P, 2, 16 * P], BF16, name="stage", tag=tag, align_bytes=64)
+            nc.sync.dma_start(
+                out=stage[:, 0, :].rearrange("q (a f) -> q a f", f=4 * P),
+                in_=w[ORDER[n]].rearrange("g (a q t) o -> q (g a) (t o)", q=P, t=4),
+            )
+            w_stage[n] = stage
+
+        param_rows = const.tile([P, P], BF16, name="param_rows")
+        nc.vector.memset(param_rows[:], 0.0)
+        nc.sync.dma_start(out=param_rows[0:ROW_DW, :], in_=b.rearrange("v g o -> (v g) o"))
+        nc.sync.dma_start(out=param_rows[ROW_DW:ROW_BN, :], in_=dw.rearrange("i j g o -> (i j g) o"))
+        nc.sync.dma_start(out=param_rows[ROW_BN:N_PARAM_ROWS, :], in_=bn.rearrange("v k g o -> (v k g) o"))
+        load_w(0)
+        load_w(1)
+        load_w(2)
+        load_x(0)
+        load_w(3)
+        load_w(4)
+        load_x(1)
+        ident_f32 = const.tile([P, P], F32, name="ident_f32")
+        make_identity(nc, ident_f32[:])
+        ident_bf16 = const.tile([P, P], BF16, name="ident_bf16")
+        make_identity(nc, ident_bf16[:])
+        zeros = const.tile([P, 2, 3 * HW], F32, name="zeros")
+        nc.vector.memset(zeros[:], 0.0)
+
+        w_codes = keep.tile([P, NV, 4, P], U32, name="w_codes", align_bytes=64)
+        w_scales = keep.tile([P, NV, 4, P], U8, name="w_scales", align_bytes=64)
+        acc = keep.tile([P, 6, 2, T * HW], F32, name="acc")
+        u4 = keep.tile([P, G, 2, T * HW], F32, name="u4")
+        y4_odd = keep.tile([P, G, 2, T * HW // 2], F32, name="y4_odd")
+        acc_pairs = acc[:].rearrange("p k n (t r q) -> p (k n) t r q", r=2, q=HW)
+        u4_by_group = u4[:].rearrange("p g n (t r q) -> p g n t r q", r=2, q=HW)
+        u4_pairs = u4[:].rearrange("p g n (t r q) -> p (g n) t r q", r=2, q=HW)
+
+        def regroup_w(n, on_scalar):
+            stage = w_stage[n]
+            dst = stage[:, 1, :].rearrange("q (m o t) -> q m o t", m=4, t=4)
+            src = stage[:, 0, :].rearrange("q (m t o) -> q m o t", m=4, t=4)
+            if on_scalar:
+                nc.scalar.copy(out=dst, in_=src)
+            else:
+                nc.vector.tensor_copy(out=dst, in_=src)
+
+        def quant_w(n):
+            v = ORDER[n]
+            nc.vector.quantize_mx(
+                out=w_codes[:, v].rearrange("q m o -> q (m o)").bitcast(FP8X4),
+                scales=w_scales[:, v].rearrange("q m o -> q (m o)"),
+                in_=w_stage[n][:, 1, :],
+            )
+
+        x_regrouped = {}
+        x_banks = {}
+        x_quantised = {}
+
+        def bank_of(j):
+            return j // 4, (j // 2) % 2, j % 2
+
+        def transpose_x(s, j):
+            g, c, nl = bank_of(j)
+            words = x_raw[s][:].bitcast(F32)
+            bank = ps_x.tile([P, 2, 2, P], F32, name="bank")
+            for h in range(2):
+                for u in range(2):
+                    lo = (2 * g + c) * PASS_WORDS
+                    nc.tensor.transpose(
+                        bank[:, h, u, :], words[:, 2 * nl + h, lo + u:lo + PASS_WORDS:2], ident_f32[:],
+                    )
+            x_banks[(s, j)] = bank
+
+        def copy_out_x(s, j):
+            g, c, nl = bank_of(j)
+            if (s, g) not in x_regrouped:
+                x_regrouped[(s, g)] = x_grouped.tile([P, 2, 4 * PASS_COLS], BF16, name="grouped", align_bytes=64)
+            words = x_regrouped[(s, g)][:].bitcast(F32)
+            nc.scalar.copy(
+                out=words[:, c, nl * 2 * SEG:(nl + 1) * 2 * SEG].rearrange("p (h r u) -> p h r u", h=2, u=2),
+                in_=x_banks[(s, j)][:].rearrange("p h u r -> p h r u"),
+            )
+
+        def quant_x(s, g):
+            codes = x_mx.tile([P, 2 * PASS_COLS], U32, name="codes", align_bytes=64)
+            scales = x_mx.tile([P, 2 * PASS_COLS], U8, name="scales", align_bytes=64)
+            nc.vector.quantize_mx(
+                out=codes[:].bitcast(FP8X4),
+                scales=scales[:],
+                in_=x_regrouped[(s, g)][:].rearrange("p a c -> p (a c)"),
+            )
+            x_quantised[(s, g)] = (codes, scales)
+
+        y_banks = {}
+        y0_normed = {}
+
+        def mx_passes(s, v):
+            for g in range(G):
+                codes, scales = x_quantised[(s, g)]
+                y = ps_y.tile([P, PASS_COLS], F32, name="y")
+                for c in range(2):
+                    nc.tensor.matmul_mx(
+                        out=y[:],
+                        lhsT=w_codes[:, v, 2 * g + c, :].bitcast(FP8X4),
+                        lhsT_scale=w_scales[:, v, 2 * g + c, :],
+                        rhs=codes[:, c * PASS_COLS:(c + 1) * PASS_COLS].bitcast(FP8X4),
+                        rhs_scale=scales[:, c * PASS_COLS:(c + 1) * PASS_COLS],
+                        start=(c == 0),
+                        stop=(c == 1),
+                    )
+                y_banks[(s, v, g)] = y
+
+        def by_batch(y):
+            return y[:].rearrange("p (n c) -> p n c", n=2)
+
+        def by_parity(y):
+            return y[:].rearrange("p (n t r q) -> p n t r q", n=2, r=2, q=HW)
+
+        def odd_times(g, first, last):
+            return y4_odd[:, g, :, first * HW:last * HW].rearrange("p n (t q) -> p n t q", q=HW)
+
+        def first_tap(s, v, g):
+            tcn = s % NCH
+            i = v - 1
+            shift = HW * v
+            if tcn < NCH - 1:
+                pieces = [(0, SEG, const_mid)]
+            else:
+                pieces = [(0, SEG - 2 * shift, const_mid), (SEG - 2 * shift, SEG - shift, const_end)]
+            for lo, hi, constant in pieces:
+                at = tcn * SEG + shift
+                nc.scalar.activation(
+                    out=acc[:, 2 * i + g, :, at + lo:at + hi], in_=by_batch(y_banks[(s, v, g)])[:, :, lo:hi],
+                    func=ACT.Identity, scale=taps_scaled[:, i, 0, g:g + 1], bias=constant[:, i, g:g + 1],
+                )
+
+        def first_read(s, v):
+            t0 = (s % NCH) * NH
+            if v == 0:
+                y0_normed[s] = normed0.tile([P, G, PASS_COLS], F32, name="normed")
+            for g in range(G):
+                if v == 0:
+                    nc.scalar.activation(
+                        out=y0_normed[s][:, g, :], in_=y_banks[(s, v, g)][:], func=ACT.Identity,
+                        scale=bn_scale[:, 0, g:g + 1], bias=bn_const[:, 0, g:g + 1],
+                    )
+                elif v == 4:
+                    nc.scalar.copy(out=odd_times(g, t0, t0 + NH), in_=by_parity(y_banks[(s, v, g)])[:, :, :, 1, :])
+                else:
+                    first_tap(s, v, g)
+
+        def other_reads(s, v):
+            tcn = s % NCH
+            t0 = tcn * NH
+            if v == 0:
+                return
+            if v == 4:
+                skip = 1 if tcn == 0 else 0
+                for g in range(G):
+                    nc.vector.tensor_tensor(
+                        out=u4_by_group[:, g, :, t0:t0 + NH, 0, :], in0=by_parity(y_banks[(s, v, g)])[:, :, :, 0, :],
+                        in1=odd_times(g, t0, t0 + NH), op=ALU.max,
+                    )
+                for g in range(G):
+                    nc.vector.tensor_tensor(
+                        out=u4_by_group[:, g, :, t0 + skip - 1:t0 + NH - 1, 1, :],
+                        in0=by_parity(y_banks[(s, v, g)])[:, :, skip:NH, 0, :],
+                        in1=odd_times(g, t0 + skip - 1, t0 + NH - 1), op=ALU.max,
+                    )
+                if tcn == NCH - 1:
+                    nc.vector.tensor_copy(
+                        out=u4_pairs[:, :, T // 2 - 1, 1, :],
+                        in_=y4_odd[:].rearrange("p g n c -> p (g n) c")[:, :, (T // 2 - 1) * HW:(T // 2) * HW],
+                    )
+                return
+            i = v - 1
+            shift = HW * v
+            skip = shift if tcn == 0 else 0
+            if tcn == 0:
+                for g in range(G):
+                    nc.vector.tensor_scalar(
+                        out=acc[:, 2 * i + g, :, 0:shift], in0=zeros[:, :, 0:shift],
+                        scalar1=const_start[:, i, g:g + 1], scalar2=None, op0=ALU.add,
+                    )
+            for j, lo in ((1, 0), (2, skip)):
+                at = tcn * SEG - (j - 1) * shift
+                for g in range(G):
+                    cells = acc[:, 2 * i + g, :, at + lo:at + SEG]
+                    nc.vector.scalar_tensor_tensor(
+                        out=cells, in0=by_batch(y_banks[(s, v, g)])[:, :, lo:SEG], scalar=taps_scaled[:, i, j, g:g + 1],
+                        in1=cells, op0=ALU.mult, op1=ALU.add,
+                    )
+
+        pooled = {}
+        back_banks = {}
+        out_rows = {}
+        branches_done = {}
+
+        def norm4(s, g):
+            at = (s % NCH) * SEG
+            cells = u4[:, g, :, at:at + SEG]
+            if g == 0:
+                nc.scalar.activation(
+                    out=cells, in_=cells, func=ACT.Identity, scale=bn_scale[:, 4, g:g + 1], bias=bn_const[:, 4, g:g + 1],
+                )
+            else:
+                nc.gpsimd.tensor_scalar(
+                    out=cells, in0=cells, scalar1=bn_scale[:, 4, g:g + 1], scalar2=bn_const[:, 4, g:g + 1],
+                    op0=ALU.mult, op1=ALU.add,
+                )
+
+        def pool_pairs(s, v):
+            t0 = (s % NCH) * NH
+            if s not in pooled:
+                pooled[s] = pooled_pool.tile([P, G * NV, SEG], F32, name="pooled", tag="pooled", align_bytes=64)
+            if v == 0:
+                pairs = y0_normed[s][:].rearrange("p g (n t r q) -> p (g n) t r q", n=2, r=2, q=HW)
+            elif v == 4:
+                pairs = u4_pairs[:, :, t0:t0 + NH]
+            else:
+                pairs = acc_pairs[:, 4 * (v - 1):4 * v, t0:t0 + NH]
+            nc.vector.tensor_tensor(
+                out=pooled[s][:, 2 * v:2 * v + 2, :].rearrange("p g (n t q) -> p (g n) t q", n=2, q=HW),
+                in0=pairs[:, :, :, 0, :], in1=pairs[:, :, :, 1, :], op=ALU.max,
+            )
+
+        def transpose_back(s, v):
+            bank = ps_back.tile([P, 2, 2, P], F32, name="back", tag="back")
+            for nl in range(2):
+                for g in range(G):
+                    nc.tensor.transpose(bank[:, nl, g, :], pooled[s][:, 2 * v + g, nl * P:(nl + 1) * P], ident_f32[:])
+            back_banks[(s, v)] = bank
+
+        def relu_and_store(s, v):
+            pair, tcn = divmod(s, NCH)
+            by_branch = s >= STORE_BY_BRANCH_FROM
+            if by_branch:
+                small = out_small.tile([P, 2, OUT_V], F32, name="small")
+                dst = small[:]
+            else:
+                if s not in out_rows:
+                    out_rows[s] = out_pool.tile([P, 2, NV * OUT_V], F32, name="out_rows", tag="out_rows", align_bytes=64)
+                    branches_done[s] = 0
+                dst = out_rows[s][:, :, v * OUT_V:(v + 1) * OUT_V]
+            nc.scalar.activation(
+                out=dst.rearrange("p n (o g) -> p n o g", g=2),
+                in_=back_banks[(s, v)][:].rearrange("p n g o -> p n o g"), func=ACT.Relu,
+            )
+            rows = [out[2 * pair + nl, tcn * NH:(tcn + 1) * NH].rearrange("t p q c -> (t p q) c") for nl in range(2)]
+            if by_branch:
+                for nl in range(2):
+                    nc.sync.dma_start(out=rows[nl][:, v * OUT_V:(v + 1) * OUT_V], in_=small[:, nl, :])
+                return
+            branches_done[s] = branches_done[s] + 1
+            if branches_done[s] == NV:
+                for nl in range(2):
+                    nc.sync.dma_start(out=rows[nl], in_=out_rows[s][:, nl, :])
+
+        def put(table, slot, item):
+            table[slot] = table.get(slot, []) + [item]
+
+        x_stage_at = {}
+        quant_at = {}
+        load_at = {}
+        norm4_at = {}
+        pool_at = {}
+        back_at = {}
+        x_stage_end = {0: -1}
+        for c in range(1, NSTEP):
+            first = NV * (c - 1) - X_AHEAD[c]
+            for pair_of_banks in range(4):
+                put(x_stage_at, first + pair_of_banks, (c, pair_of_banks))
+            put(quant_at, first + 2, (c, 0))
+            put(quant_at, first + 3, (c, 1))
+            x_stage_end[c] = first + 3
+        for c in range(2, NSTEP):
+            put(load_at, max(0, x_stage_end[c - 2] + 1), c)
+        for unit in range(NU):
+            s, v = unit // NV, ORDER[unit % NV]
+            complete = unit + NV if (s < NSTEP - 1 and v != 0) else unit
+            put(pool_at, complete + POOL_LAG[v], (s, v))
+            put(back_at, complete + POOL_LAG[v] + BACK_LAG, (s, v))
+            if v == 4:
+                put(norm4_at, complete, s)
+
+        regroup_w(0, False)
+        regroup_w(1, True)
+        regroup_w(2, False)
+        quant_w(0)
+        quant_w(1)
+        quant_w(2)
+
+        params_t = ps_back.tile([P, P], BF16, name="params_t", tag="back")
+        nc.tensor.transpose(params_t[:], param_rows[:], ident_bf16[:])
+        params = const.tile([P, N_PARAM_ROWS], F32, name="params")
+        nc.vector.tensor_copy(out=params[:], in_=params_t[:, 0:N_PARAM_ROWS])
+        bias = params[:, 0:ROW_DW].rearrange("p (v g) -> p v g", g=2)
+        taps = params[:, ROW_DW:ROW_BN].rearrange("p (i j g) -> p i j g", j=3, g=2)
+        bn_rows = params[:, ROW_BN:N_PARAM_ROWS].rearrange("p (v k g) -> p v k g", k=4, g=2)
+
+        var_eps = const.tile([P, NV, G], F32, name="var_eps")
+        rstd = const.tile([P, NV, G], F32, name="rstd")
+        work = const.tile([P, NV, G], F32, name="work")
+        bn_scale = const.tile([P, NV, G], F32, name="bn_scale")
+        bn_shift = const.tile([P, NV, G], F32, name="bn_shift")
+        bn_const = const.tile([P, NV, G], F32, name="bn_const")
+        nc.vector.tensor_scalar_add(out=var_eps[:], in0=bn_rows[:, :, 3, :], scalar1=EPS)
+        nc.scalar.sqrt(out=rstd[:], in_=var_eps[:])
+        nc.vector.reciprocal(out=rstd[:], in_=rstd[:])
+        nc.vector.tensor_mul(out=work[:], in0=rstd[:], in1=rstd[:])
+        nc.vector.tensor_mul(out=work[:], in0=work[:], in1=var_eps[:])
+        nc.vector.tensor_scalar(out=work[:], in0=work[:], scalar1=-0.5, scalar2=1.5, op0=ALU.mult, op1=ALU.add)
+        nc.vector.tensor_mul(out=rstd[:], in0=rstd[:], in1=work[:])
+        nc.vector.tensor_mul(out=bn_scale[:], in0=rstd[:], in1=bn_rows[:, :, 0, :])
+        nc.vector.tensor_mul(out=work[:], in0=bn_scale[:], in1=bn_rows[:, :, 2, :])
+        nc.vector.tensor_sub(out=bn_shift[:], in0=bn_rows[:, :, 1, :], in1=work[:])
+        nc.vector.tensor_mul(out=work[:], in0=bn_scale[:], in1=bias)
+        nc.vector.tensor_add(out=bn_const[:], in0=bn_shift[:], in1=work[:])
+        taps_scaled = const.tile([P, 3, 3, G], F32, name="taps_scaled")
+        tap_bias = const.tile([P, 3, 3, G], F32, name="tap_bias")
+        for j in range(3):
+            nc.vector.tensor_mul(out=taps_scaled[:, :, j, :], in0=taps[:, :, j, :], in1=bn_scale[:, 1:4, :])
+        for j in range(3):
+            nc.vector.tensor_mul(out=tap_bias[:, :, j, :], in0=taps_scaled[:, :, j, :], in1=bias[:, 1:4, :])
+        const_end = const.tile([P, 3, G], F32, name="const_end")
+        const_mid = const.tile([P, 3, G], F32, name="const_mid")
+        const_start = const.tile([P, 3, G], F32, name="const_start")
+        nc.vector.tensor_add(out=const_start[:], in0=bn_shift[:, 1:4, :], in1=tap_bias[:, :, 1, :])
+        nc.vector.tensor_add(out=const_end[:], in0=const_start[:], in1=tap_bias[:, :, 0, :])
+        nc.vector.tensor_add(out=const_mid[:], in0=const_end[:], in1=tap_bias[:, :, 2, :])
+        nc.vector.tensor_add(out=const_start[:], in0=const_start[:], in1=tap_bias[:, :, 2, :])
+
+        regroup_w(3, False)
+        for j in range(8):
+            transpose_x(0, j)
+            copy_out_x(0, j)
+            if j == 5:
+                quant_x(0, 0)
+                quant_w(3)
+        quant_x(0, 1)
+
+        last_slot = max(back_at)
+        for slot in range(last_slot + 1):
+            s, v = slot // NV, ORDER[slot % NV]
+            has_unit = slot < NU
+            x_pairs = x_stage_at.get(slot, [])
+            for c in load_at.get(slot, []):
+                load_x(c)
+            if has_unit:
+                mx_passes(s, v)
+            for c, pair_of_banks in x_pairs[:1]:
+                transpose_x(c, 2 * pair_of_banks)
+                transpose_x(c, 2 * pair_of_banks + 1)
+            for chunk, branch in back_at.get(slot, []):
+                transpose_back(chunk, branch)
+            if has_unit:
+                first_read(s, v)
+            for chunk in norm4_at.get(slot - 1, []):
+                norm4(chunk, 0)
+            if has_unit:
+                other_reads(s, v)
+            for chunk in norm4_at.get(slot, []):
+                norm4(chunk, 1)
+            for chunk, branch in pool_at.get(slot, []):
+                pool_pairs(chunk, branch)
+            for n, (c, pair_of_banks) in enumerate(x_pairs):
+                if n > 0:
+                    transpose_x(c, 2 * pair_of_banks)
+                    transpose_x(c, 2 * pair_of_banks + 1)
+                copy_out_x(c, 2 * pair_of_banks)
+                copy_out_x(c, 2 * pair_of_banks + 1)
+            for chunk, branch in back_at.get(slot, []):
+                relu_and_store(chunk, branch)
+            for c, g in quant_at.get(slot, []):
+                quant_x(c, g)
+            if slot == 0:
+                regroup_w(4, False)
+            if slot == 1:
+                quant_w(4)

@@ -27,7 +27,7 @@ OUT_V = G * CB
 ORDER = (4, 3, 2, 1, 0)
 NU = NSTEP * NV
 X_AHEAD = (0, 0, 2, 3, 3, 3, 3, 3)
-POOL_LAG = {0: 1, 1: 1, 2: 1, 3: 1, 4: 2}
+POOL_LAG = {0: 0, 1: 1, 2: 1, 3: 1, 4: 0}
 BACK_LAG = 2
 STORE_BY_BRANCH_FROM = NSTEP - 2
 ROW_DW = NV * G
@@ -42,10 +42,10 @@ def tile_timeception_pa_t_kernel(tc, x, w, b, dw, bn, out):
         ctx.enter_context(tc.manual_schedule())
         const = ctx.enter_context(tc.tile_pool(name="const", bufs=1))
         keep = ctx.enter_context(tc.tile_pool(name="keep", bufs=1))
-        x_in = ctx.enter_context(tc.tile_pool(name="x_in", bufs=2))
+        x_in = ctx.enter_context(tc.tile_pool(name="x_in", bufs=4))
         x_grouped = ctx.enter_context(tc.tile_pool(name="x_grouped", bufs=2))
         x_mx = ctx.enter_context(tc.tile_pool(name="x_mx", bufs=4))
-        normed0 = ctx.enter_context(tc.tile_pool(name="normed0", bufs=3))
+        short = ctx.enter_context(tc.tile_pool(name="short", bufs=2))
         out_small = ctx.enter_context(tc.tile_pool(name="out_small", bufs=2 * NV))
         pooled_pool = ctx.enter_context(tc.tile_pool(name="pooled_pool", bufs=2))
         out_pool = ctx.enter_context(tc.tile_pool(name="out_pool", bufs=2))
@@ -55,16 +55,16 @@ def tile_timeception_pa_t_kernel(tc, x, w, b, dw, bn, out):
 
         x_raw = {}
 
-        def load_x(s):
+        def load_x(s, g):
             pair, tcn = divmod(s, NCH)
-            raw = x_in.tile([P, 4, G * K], BF16, name="raw")
+            raw = x_in.tile([P, 4, K], BF16, name="raw")
             for nl in range(2):
                 src = x[2 * pair + nl, tcn * TC:(tcn + 1) * TC]
                 nc.sync.dma_start(
                     out=raw[:, 2 * nl:2 * nl + 2, :],
-                    in_=src.rearrange("(h t) p q c -> (t p q) h c", h=2),
+                    in_=src.rearrange("(h t) p q c -> (t p q) h c", h=2)[:, :, g * K:(g + 1) * K],
                 )
-            x_raw[s] = raw
+            x_raw[(s, g)] = raw
 
         w_stage = {}
 
@@ -79,40 +79,46 @@ def tile_timeception_pa_t_kernel(tc, x, w, b, dw, bn, out):
 
         param_rows = const.tile([P, P], BF16, name="param_rows")
         nc.vector.memset(param_rows[:], 0.0)
-        nc.sync.dma_start(out=param_rows[0:ROW_DW, :], in_=b.rearrange("v g o -> (v g) o"))
-        nc.sync.dma_start(out=param_rows[ROW_DW:ROW_BN, :], in_=dw.rearrange("i j g o -> (i j g) o"))
+        zeros = const.tile([P, 2, 3 * HW], F32, name="zeros")
+        nc.vector.memset(zeros[:], 0.0)
+        spare = const.tile([P, 1], F32, name="spare")
+        nc.scalar.copy(out=spare[:], in_=zeros[:, 0, 0:1])
+        load_x(0, 0)
         nc.sync.dma_start(out=param_rows[ROW_BN:N_PARAM_ROWS, :], in_=bn.rearrange("v k g o -> (v k g) o"))
+        nc.sync.dma_start(out=param_rows[ROW_DW:ROW_BN, :], in_=dw.rearrange("i j g o -> (i j g) o"))
+        nc.sync.dma_start(out=param_rows[0:ROW_DW, :], in_=b.rearrange("v g o -> (v g) o"))
         load_w(0)
+        load_x(0, 1)
         load_w(1)
         load_w(2)
-        load_x(0)
+        load_x(1, 0)
         load_w(3)
+        load_x(1, 1)
         load_w(4)
-        load_x(1)
         ident_f32 = const.tile([P, P], F32, name="ident_f32")
         make_identity(nc, ident_f32[:])
         ident_bf16 = const.tile([P, P], BF16, name="ident_bf16")
         make_identity(nc, ident_bf16[:])
-        zeros = const.tile([P, 2, 3 * HW], F32, name="zeros")
-        nc.vector.memset(zeros[:], 0.0)
 
         w_codes = keep.tile([P, NV, 4, P], U32, name="w_codes", align_bytes=64)
         w_scales = keep.tile([P, NV, 4, P], U8, name="w_scales", align_bytes=64)
         acc = keep.tile([P, 6, 2, T * HW], F32, name="acc")
-        u4 = keep.tile([P, G, 2, T * HW], F32, name="u4")
-        y4_odd = keep.tile([P, G, 2, T * HW // 2], F32, name="y4_odd")
+        even4 = keep.tile([P, G, 2, (T // 2 + 1) * HW], F32, name="even4")
+        early_cells = even4[:, :, :, 0:T // 2 * HW].rearrange("p g n (k c) -> p (g n) k c", k=NCH)[:, :, 1:, 0:HW]
+        nc.gpsimd.memset(early_cells, 0.0)
+        last4 = keep.tile([P, 2, G, 2, HW], F32, name="last4")
         acc_pairs = acc[:].rearrange("p k n (t r q) -> p (k n) t r q", r=2, q=HW)
-        u4_by_group = u4[:].rearrange("p g n (t r q) -> p g n t r q", r=2, q=HW)
-        u4_pairs = u4[:].rearrange("p g n (t r q) -> p (g n) t r q", r=2, q=HW)
 
-        def regroup_w(n, on_scalar):
+        def regroup_w(n, engine):
             stage = w_stage[n]
             dst = stage[:, 1, :].rearrange("q (m o t) -> q m o t", m=4, t=4)
             src = stage[:, 0, :].rearrange("q (m t o) -> q m o t", m=4, t=4)
-            if on_scalar:
+            if engine == "scalar":
                 nc.scalar.copy(out=dst, in_=src)
-            else:
+            elif engine == "vector":
                 nc.vector.tensor_copy(out=dst, in_=src)
+            else:
+                nc.gpsimd.tensor_scalar(out=dst, in0=src, scalar1=1.0, scalar2=0.0, op0=ALU.mult, op1=ALU.add)
 
         def quant_w(n):
             v = ORDER[n]
@@ -129,13 +135,13 @@ def tile_timeception_pa_t_kernel(tc, x, w, b, dw, bn, out):
         def bank_of(j):
             return j // 4, (j // 2) % 2, j % 2
 
-        def transpose_x(s, j):
+        def transpose_x(s, j, pool=ps_x, tag="bank"):
             g, c, nl = bank_of(j)
-            words = x_raw[s][:].bitcast(F32)
-            bank = ps_x.tile([P, 2, 2, P], F32, name="bank")
+            words = x_raw[(s, g)][:].bitcast(F32)
+            bank = pool.tile([P, 2, 2, P], F32, name="bank", tag=tag)
             for h in range(2):
                 for u in range(2):
-                    lo = (2 * g + c) * PASS_WORDS
+                    lo = c * PASS_WORDS
                     nc.tensor.transpose(
                         bank[:, h, u, :], words[:, 2 * nl + h, lo + u:lo + PASS_WORDS:2], ident_f32[:],
                     )
@@ -146,10 +152,9 @@ def tile_timeception_pa_t_kernel(tc, x, w, b, dw, bn, out):
             if (s, g) not in x_regrouped:
                 x_regrouped[(s, g)] = x_grouped.tile([P, 2, 4 * PASS_COLS], BF16, name="grouped", align_bytes=64)
             words = x_regrouped[(s, g)][:].bitcast(F32)
-            nc.scalar.copy(
-                out=words[:, c, nl * 2 * SEG:(nl + 1) * 2 * SEG].rearrange("p (h r u) -> p h r u", h=2, u=2),
-                in_=x_banks[(s, j)][:].rearrange("p h u r -> p h r u"),
-            )
+            dst = words[:, c, nl * 2 * SEG:(nl + 1) * 2 * SEG].rearrange("p (h r u) -> p h r u", h=2, u=2)
+            src = x_banks[(s, j)][:].rearrange("p h u r -> p h r u")
+            nc.scalar.copy(out=dst, in_=src)
 
         def quant_x(s, g):
             codes = x_mx.tile([P, 2 * PASS_COLS], U32, name="codes", align_bytes=64)
@@ -162,7 +167,8 @@ def tile_timeception_pa_t_kernel(tc, x, w, b, dw, bn, out):
             x_quantised[(s, g)] = (codes, scales)
 
         y_banks = {}
-        y0_normed = {}
+        best0 = {}
+        best4 = {}
 
         def mx_passes(s, v):
             for g in range(G):
@@ -186,8 +192,8 @@ def tile_timeception_pa_t_kernel(tc, x, w, b, dw, bn, out):
         def by_parity(y):
             return y[:].rearrange("p (n t r q) -> p n t r q", n=2, r=2, q=HW)
 
-        def odd_times(g, first, last):
-            return y4_odd[:, g, :, first * HW:last * HW].rearrange("p n (t q) -> p n t q", q=HW)
+        def by_time(cells):
+            return cells.rearrange("p n (t q) -> p n t q", q=HW)
 
         def first_tap(s, v, g):
             tcn = s % NCH
@@ -204,54 +210,76 @@ def tile_timeception_pa_t_kernel(tc, x, w, b, dw, bn, out):
                     func=ACT.Identity, scale=taps_scaled[:, i, 0, g:g + 1], bias=constant[:, i, g:g + 1],
                 )
 
+        def start_acc():
+            for i in reversed(range(3)):
+                for g in range(G):
+                    nc.gpsimd.tensor_scalar(
+                        out=acc[:, 2 * i + g, :, 0:(i + 1) * HW], in0=zeros[:, :, 0:(i + 1) * HW],
+                        scalar1=zeros[:, 0, 0:1], scalar2=const_start[:, i, g:g + 1], op0=ALU.mult, op1=ALU.add,
+                    )
+
         def first_read(s, v):
             t0 = (s % NCH) * NH
             if v == 0:
-                y0_normed[s] = normed0.tile([P, G, PASS_COLS], F32, name="normed")
+                best0[s] = short.tile([P, G, 2, NH * HW], F32, name="best0")
             for g in range(G):
+                y = by_parity(y_banks[(s, v, g)])
                 if v == 0:
                     nc.scalar.activation(
-                        out=y0_normed[s][:, g, :], in_=y_banks[(s, v, g)][:], func=ACT.Identity,
-                        scale=bn_scale[:, 0, g:g + 1], bias=bn_const[:, 0, g:g + 1],
+                        out=by_time(best0[s][:, g]), in_=y[:, :, :, 1, :], func=ACT.Copy, scale=sign[:, 0, g:g + 1],
                     )
                 elif v == 4:
-                    nc.scalar.copy(out=odd_times(g, t0, t0 + NH), in_=by_parity(y_banks[(s, v, g)])[:, :, :, 1, :])
+                    nc.scalar.activation(
+                        out=by_time(even4[:, g, :, t0 * HW:(t0 + NH) * HW]), in_=y[:, :, :, 0, :], func=ACT.Copy,
+                        scale=sign[:, 4, g:g + 1],
+                    )
                 else:
                     first_tap(s, v, g)
+            if v == 4:
+                for g in range(G):
+                    y_last = by_parity(y_banks[(s, v, g)])[:, :, NH - 1, 1, :]
+                    if s % NCH < NCH - 1:
+                        nc.scalar.copy(out=last4[:, s % 2, g], in_=y_last)
+                    else:
+                        nc.scalar.activation(
+                            out=even4[:, g, :, T // 2 * HW:], in_=y_last, func=ACT.Copy, scale=sign[:, 4, g:g + 1],
+                        )
 
         def other_reads(s, v):
             tcn = s % NCH
             t0 = tcn * NH
             if v == 0:
+                for g in range(G):
+                    nc.vector.scalar_tensor_tensor(
+                        out=by_time(best0[s][:, g]), in0=by_parity(y_banks[(s, v, g)])[:, :, :, 0, :],
+                        scalar=sign[:, 0, g:g + 1], in1=by_time(best0[s][:, g]), op0=ALU.mult, op1=ALU.max,
+                    )
                 return
             if v == 4:
-                skip = 1 if tcn == 0 else 0
+                first = t0 if tcn == 0 else t0 - 1
+                end = t0 + NH
+                neighbours = short.tile([P, G, 2, (NH + 1) * HW], F32, name="neighbours")
+                nc.vector.tensor_tensor(
+                    out=neighbours[:, :, :, (first - t0 + 1) * HW:(end - t0 + 1) * HW].rearrange("p g n c -> p (g n) c"),
+                    in0=even4[:, :, :, first * HW:end * HW].rearrange("p g n c -> p (g n) c"),
+                    in1=even4[:, :, :, (first + 1) * HW:(end + 1) * HW].rearrange("p g n c -> p (g n) c"), op=ALU.max,
+                )
+                best4[s] = short.tile([P, G, 2, NH * HW], F32, name="best4")
                 for g in range(G):
-                    nc.vector.tensor_tensor(
-                        out=u4_by_group[:, g, :, t0:t0 + NH, 0, :], in0=by_parity(y_banks[(s, v, g)])[:, :, :, 0, :],
-                        in1=odd_times(g, t0, t0 + NH), op=ALU.max,
+                    nc.vector.scalar_tensor_tensor(
+                        out=by_time(best4[s][:, g]), in0=by_time(neighbours[:, g, :, HW:]), scalar=sign[:, 4, g:g + 1],
+                        in1=by_parity(y_banks[(s, v, g)])[:, :, :, 1, :], op0=ALU.mult, op1=ALU.max,
                     )
-                for g in range(G):
-                    nc.vector.tensor_tensor(
-                        out=u4_by_group[:, g, :, t0 + skip - 1:t0 + NH - 1, 1, :],
-                        in0=by_parity(y_banks[(s, v, g)])[:, :, skip:NH, 0, :],
-                        in1=odd_times(g, t0 + skip - 1, t0 + NH - 1), op=ALU.max,
-                    )
-                if tcn == NCH - 1:
-                    nc.vector.tensor_copy(
-                        out=u4_pairs[:, :, T // 2 - 1, 1, :],
-                        in_=y4_odd[:].rearrange("p g n c -> p (g n) c")[:, :, (T // 2 - 1) * HW:(T // 2) * HW],
-                    )
+                if tcn > 0:
+                    for g in range(G):
+                        nc.vector.scalar_tensor_tensor(
+                            out=best4[s - 1][:, g, :, (NH - 1) * HW:], in0=neighbours[:, g, :, 0:HW],
+                            scalar=sign[:, 4, g:g + 1], in1=last4[:, (s - 1) % 2, g], op0=ALU.mult, op1=ALU.max,
+                        )
                 return
             i = v - 1
             shift = HW * v
             skip = shift if tcn == 0 else 0
-            if tcn == 0:
-                for g in range(G):
-                    nc.vector.tensor_scalar(
-                        out=acc[:, 2 * i + g, :, 0:shift], in0=zeros[:, :, 0:shift],
-                        scalar1=const_start[:, i, g:g + 1], scalar2=None, op0=ALU.add,
-                    )
             for j, lo in ((1, 0), (2, skip)):
                 at = tcn * SEG - (j - 1) * shift
                 for g in range(G):
@@ -266,29 +294,20 @@ def tile_timeception_pa_t_kernel(tc, x, w, b, dw, bn, out):
         out_rows = {}
         branches_done = {}
 
-        def norm4(s, g):
-            at = (s % NCH) * SEG
-            cells = u4[:, g, :, at:at + SEG]
-            if g == 0:
-                nc.scalar.activation(
-                    out=cells, in_=cells, func=ACT.Identity, scale=bn_scale[:, 4, g:g + 1], bias=bn_const[:, 4, g:g + 1],
-                )
-            else:
-                nc.gpsimd.tensor_scalar(
-                    out=cells, in0=cells, scalar1=bn_scale[:, 4, g:g + 1], scalar2=bn_const[:, 4, g:g + 1],
-                    op0=ALU.mult, op1=ALU.add,
-                )
-
         def pool_pairs(s, v):
             t0 = (s % NCH) * NH
             if s not in pooled:
                 pooled[s] = pooled_pool.tile([P, G * NV, SEG], F32, name="pooled", tag="pooled", align_bytes=64)
-            if v == 0:
-                pairs = y0_normed[s][:].rearrange("p g (n t r q) -> p (g n) t r q", n=2, r=2, q=HW)
-            elif v == 4:
-                pairs = u4_pairs[:, :, t0:t0 + NH]
-            else:
-                pairs = acc_pairs[:, 4 * (v - 1):4 * v, t0:t0 + NH]
+            if v in (0, 4):
+                best, scale = (best0, abs_scale0[:]) if v == 0 else (best4, bn_scale[:, 4, :])
+                engine = nc.vector if (s, v) == (NSTEP - 1, 0) else nc.gpsimd
+                for g in range(G):
+                    engine.tensor_scalar(
+                        out=pooled[s][:, 2 * v + g, :], in0=best[s][:, g].rearrange("p n c -> p (n c)"),
+                        scalar1=scale[:, g:g + 1], scalar2=bn_const[:, v, g:g + 1], op0=ALU.mult, op1=ALU.add,
+                    )
+                return
+            pairs = acc_pairs[:, 4 * (v - 1):4 * v, t0:t0 + NH]
             nc.vector.tensor_tensor(
                 out=pooled[s][:, 2 * v:2 * v + 2, :].rearrange("p g (n t q) -> p (g n) t q", n=2, q=HW),
                 in0=pairs[:, :, :, 0, :], in1=pairs[:, :, :, 1, :], op=ALU.max,
@@ -332,7 +351,6 @@ def tile_timeception_pa_t_kernel(tc, x, w, b, dw, bn, out):
         x_stage_at = {}
         quant_at = {}
         load_at = {}
-        norm4_at = {}
         pool_at = {}
         back_at = {}
         x_stage_end = {0: -1}
@@ -350,64 +368,73 @@ def tile_timeception_pa_t_kernel(tc, x, w, b, dw, bn, out):
             complete = unit + NV if (s < NSTEP - 1 and v != 0) else unit
             put(pool_at, complete + POOL_LAG[v], (s, v))
             put(back_at, complete + POOL_LAG[v] + BACK_LAG, (s, v))
-            if v == 4:
-                put(norm4_at, complete, s)
+        pool_at[NU - 1] = sorted(pool_at[NU - 1])
+        back_at[NU - 1 + BACK_LAG] = sorted(back_at[NU - 1 + BACK_LAG])
 
-        regroup_w(0, False)
-        regroup_w(1, True)
-        regroup_w(2, False)
-        quant_w(0)
-        quant_w(1)
-        quant_w(2)
-
-        params_t = ps_back.tile([P, P], BF16, name="params_t", tag="back")
-        nc.tensor.transpose(params_t[:], param_rows[:], ident_bf16[:])
+        params_bank = ps_back.tile([P, P], BF16, name="params_bank", tag="back")
         params = const.tile([P, N_PARAM_ROWS], F32, name="params")
-        nc.vector.tensor_copy(out=params[:], in_=params_t[:, 0:N_PARAM_ROWS])
+        for nl in range(2):
+            for c in range(2):
+                transpose_x(0, 2 * c + nl, ps_y, "y")
+                copy_out_x(0, 2 * c + nl)
+            if nl == 0:
+                nc.tensor.transpose(params_bank[:], param_rows[:], ident_bf16[:])
+                nc.vector.tensor_copy(out=params[:], in_=params_bank[:, 0:N_PARAM_ROWS])
+
         bias = params[:, 0:ROW_DW].rearrange("p (v g) -> p v g", g=2)
         taps = params[:, ROW_DW:ROW_BN].rearrange("p (i j g) -> p i j g", j=3, g=2)
         bn_rows = params[:, ROW_BN:N_PARAM_ROWS].rearrange("p (v k g) -> p v k g", k=4, g=2)
 
+        minus_half = const.tile([P, NV, G], F32, name="minus_half")
         var_eps = const.tile([P, NV, G], F32, name="var_eps")
         rstd = const.tile([P, NV, G], F32, name="rstd")
         work = const.tile([P, NV, G], F32, name="work")
         bn_scale = const.tile([P, NV, G], F32, name="bn_scale")
         bn_shift = const.tile([P, NV, G], F32, name="bn_shift")
         bn_const = const.tile([P, NV, G], F32, name="bn_const")
-        nc.vector.tensor_scalar_add(out=var_eps[:], in0=bn_rows[:, :, 3, :], scalar1=EPS)
-        nc.scalar.sqrt(out=rstd[:], in_=var_eps[:])
-        nc.vector.reciprocal(out=rstd[:], in_=rstd[:])
-        nc.vector.tensor_mul(out=work[:], in0=rstd[:], in1=rstd[:])
-        nc.vector.tensor_mul(out=work[:], in0=work[:], in1=var_eps[:])
-        nc.vector.tensor_scalar(out=work[:], in0=work[:], scalar1=-0.5, scalar2=1.5, op0=ALU.mult, op1=ALU.add)
-        nc.vector.tensor_mul(out=rstd[:], in0=rstd[:], in1=work[:])
-        nc.vector.tensor_mul(out=bn_scale[:], in0=rstd[:], in1=bn_rows[:, :, 0, :])
-        nc.vector.tensor_mul(out=work[:], in0=bn_scale[:], in1=bn_rows[:, :, 2, :])
-        nc.vector.tensor_sub(out=bn_shift[:], in0=bn_rows[:, :, 1, :], in1=work[:])
-        nc.vector.tensor_mul(out=work[:], in0=bn_scale[:], in1=bias)
-        nc.vector.tensor_add(out=bn_const[:], in0=bn_shift[:], in1=work[:])
+        sign = const.tile([P, NV, G], F32, name="sign")
+        abs_scale0 = const.tile([P, G], F32, name="abs_scale0")
         taps_scaled = const.tile([P, 3, 3, G], F32, name="taps_scaled")
         tap_bias = const.tile([P, 3, 3, G], F32, name="tap_bias")
-        for j in range(3):
-            nc.vector.tensor_mul(out=taps_scaled[:, :, j, :], in0=taps[:, :, j, :], in1=bn_scale[:, 1:4, :])
-        for j in range(3):
-            nc.vector.tensor_mul(out=tap_bias[:, :, j, :], in0=taps_scaled[:, :, j, :], in1=bias[:, 1:4, :])
         const_end = const.tile([P, 3, G], F32, name="const_end")
         const_mid = const.tile([P, 3, G], F32, name="const_mid")
         const_start = const.tile([P, 3, G], F32, name="const_start")
-        nc.vector.tensor_add(out=const_start[:], in0=bn_shift[:, 1:4, :], in1=tap_bias[:, :, 1, :])
-        nc.vector.tensor_add(out=const_end[:], in0=const_start[:], in1=tap_bias[:, :, 0, :])
-        nc.vector.tensor_add(out=const_mid[:], in0=const_end[:], in1=tap_bias[:, :, 2, :])
-        nc.vector.tensor_add(out=const_start[:], in0=const_start[:], in1=tap_bias[:, :, 2, :])
+        nc.gpsimd.memset(minus_half[:], -0.5)
+        nc.gpsimd.tensor_scalar(
+            out=sign[:], in0=bn_rows[:, :, 0, :], scalar1=0.0, scalar2=2.0, op0=ALU.is_ge, op1=ALU.mult,
+        )
+        nc.gpsimd.tensor_scalar_add(out=sign[:], in0=sign[:], scalar1=-1.0)
+        nc.gpsimd.tensor_scalar_add(out=var_eps[:], in0=bn_rows[:, :, 3, :], scalar1=EPS)
+        nc.gpsimd.tensor_tensor(out=rstd[:], in0=var_eps[:], in1=minus_half[:], op=ALU.pow)
+        nc.gpsimd.tensor_mul(out=bn_scale[:], in0=rstd[:], in1=bn_rows[:, :, 0, :])
+        nc.gpsimd.tensor_mul(out=work[:], in0=bn_scale[:], in1=bn_rows[:, :, 2, :])
+        nc.gpsimd.tensor_sub(out=bn_shift[:], in0=bn_rows[:, :, 1, :], in1=work[:])
+        def for_each_tap(values):
+            return values[:, 1:4, :].unsqueeze(2).to_broadcast([P, 3, 3, G])
 
-        regroup_w(3, False)
-        for j in range(8):
-            transpose_x(0, j)
-            copy_out_x(0, j)
-            if j == 5:
-                quant_x(0, 0)
-                quant_w(3)
+        nc.gpsimd.tensor_mul(out=taps_scaled[:], in0=taps, in1=for_each_tap(bn_scale))
+        nc.gpsimd.tensor_mul(out=tap_bias[:], in0=taps_scaled[:], in1=for_each_tap(bias))
+        nc.gpsimd.tensor_add(out=const_start[:], in0=bn_shift[:, 1:4, :], in1=tap_bias[:, :, 1, :])
+        nc.gpsimd.tensor_add(out=const_end[:], in0=const_start[:], in1=tap_bias[:, :, 0, :])
+        nc.gpsimd.tensor_add(out=const_mid[:], in0=const_end[:], in1=tap_bias[:, :, 2, :])
+        nc.gpsimd.tensor_add(out=const_start[:], in0=const_start[:], in1=tap_bias[:, :, 2, :])
+        nc.gpsimd.tensor_mul(out=work[:], in0=bn_scale[:], in1=bias)
+        nc.gpsimd.tensor_add(out=bn_const[:], in0=bn_shift[:], in1=work[:])
+        nc.gpsimd.tensor_mul(out=abs_scale0[:], in0=sign[:, 0, :], in1=bn_scale[:, 0, :])
+        start_acc()
+
+        regroup_w(0, "vector")
+        quant_x(0, 0)
+        quant_w(0)
+        for nl in range(2):
+            for c in range(2):
+                pool, tag = (ps_x, "bank") if nl == 0 else (ps_back, "back")
+                transpose_x(0, 4 + 2 * c + nl, pool, tag)
+                copy_out_x(0, 4 + 2 * c + nl)
+        regroup_w(1, "vector")
         quant_x(0, 1)
+        regroup_w(2, "scalar")
+        regroup_w(4, "gpsimd")
 
         last_slot = max(back_at)
         for slot in range(last_slot + 1):
@@ -415,7 +442,8 @@ def tile_timeception_pa_t_kernel(tc, x, w, b, dw, bn, out):
             has_unit = slot < NU
             x_pairs = x_stage_at.get(slot, [])
             for c in load_at.get(slot, []):
-                load_x(c)
+                for g in range(G):
+                    load_x(c, g)
             if has_unit:
                 mx_passes(s, v)
             for c, pair_of_banks in x_pairs[:1]:
@@ -425,12 +453,12 @@ def tile_timeception_pa_t_kernel(tc, x, w, b, dw, bn, out):
                 transpose_back(chunk, branch)
             if has_unit:
                 first_read(s, v)
-            for chunk in norm4_at.get(slot - 1, []):
-                norm4(chunk, 0)
+            if slot < NV - 1:
+                quant_w(slot + 1)
             if has_unit:
                 other_reads(s, v)
-            for chunk in norm4_at.get(slot, []):
-                norm4(chunk, 1)
+            if slot == 1:
+                regroup_w(3, "vector")
             for chunk, branch in pool_at.get(slot, []):
                 pool_pairs(chunk, branch)
             for n, (c, pair_of_banks) in enumerate(x_pairs):
@@ -443,7 +471,5 @@ def tile_timeception_pa_t_kernel(tc, x, w, b, dw, bn, out):
                 relu_and_store(chunk, branch)
             for c, g in quant_at.get(slot, []):
                 quant_x(c, g)
-            if slot == 0:
-                regroup_w(4, False)
-            if slot == 1:
-                quant_w(4)
+            if slot == NV * (NCH - 1):
+                start_acc()

@@ -30,6 +30,7 @@ X_AHEAD = (0, 0, 2, 3, 3, 3, 3, 3)
 POOL_LAG = {0: 0, 1: 1, 2: 1, 3: 1, 4: 0}
 BACK_LAG = 2
 STORE_BY_BRANCH_FROM = NSTEP - 2
+LAST_POOLED = (NSTEP - 1, 1)
 ROW_DW = NV * G
 ROW_BN = ROW_DW + 3 * 3 * G
 N_PARAM_ROWS = ROW_BN + NV * 4 * G
@@ -46,7 +47,8 @@ def tile_timeception_pa_t_kernel(tc, x, w, b, dw, bn, out):
         x_grouped = ctx.enter_context(tc.tile_pool(name="x_grouped", bufs=2))
         x_mx = ctx.enter_context(tc.tile_pool(name="x_mx", bufs=4))
         short = ctx.enter_context(tc.tile_pool(name="short", bufs=2))
-        out_small = ctx.enter_context(tc.tile_pool(name="out_small", bufs=2 * NV))
+        out_small = ctx.enter_context(tc.tile_pool(name="out_small", bufs=2 * NV - 1))
+        out_last = ctx.enter_context(tc.tile_pool(name="out_last", bufs=2))
         pooled_pool = ctx.enter_context(tc.tile_pool(name="pooled_pool", bufs=2))
         out_pool = ctx.enter_context(tc.tile_pool(name="out_pool", bufs=2))
         ps_x = ctx.enter_context(tc.psum_pool(name="ps_x", bufs=2))
@@ -55,16 +57,17 @@ def tile_timeception_pa_t_kernel(tc, x, w, b, dw, bn, out):
 
         x_raw = {}
 
-        def load_x(s, g):
+        def load_x(s, g, batches=(0, 1)):
             pair, tcn = divmod(s, NCH)
-            raw = x_in.tile([P, 4, K], BF16, name="raw")
-            for nl in range(2):
+            if (s, g) not in x_raw:
+                x_raw[(s, g)] = x_in.tile([P, 4, K], BF16, name="raw")
+            raw = x_raw[(s, g)]
+            for nl in batches:
                 src = x[2 * pair + nl, tcn * TC:(tcn + 1) * TC]
                 nc.sync.dma_start(
                     out=raw[:, 2 * nl:2 * nl + 2, :],
                     in_=src.rearrange("(h t) p q c -> (t p q) h c", h=2)[:, :, g * K:(g + 1) * K],
                 )
-            x_raw[(s, g)] = raw
 
         w_stage = {}
 
@@ -83,13 +86,15 @@ def tile_timeception_pa_t_kernel(tc, x, w, b, dw, bn, out):
         nc.vector.memset(zeros[:], 0.0)
         spare = const.tile([P, 1], F32, name="spare")
         nc.scalar.copy(out=spare[:], in_=zeros[:, 0, 0:1])
-        load_x(0, 0)
+        load_x(0, 0, [0])
+        load_w(0)
+        load_x(0, 0, [1])
         nc.sync.dma_start(out=param_rows[ROW_BN:N_PARAM_ROWS, :], in_=bn.rearrange("v k g o -> (v k g) o"))
         nc.sync.dma_start(out=param_rows[ROW_DW:ROW_BN, :], in_=dw.rearrange("i j g o -> (i j g) o"))
         nc.sync.dma_start(out=param_rows[0:ROW_DW, :], in_=b.rearrange("v g o -> (v g) o"))
-        load_w(0)
-        load_x(0, 1)
+        load_x(0, 1, [0])
         load_w(1)
+        load_x(0, 1, [1])
         load_w(2)
         load_x(1, 0)
         load_w(3)
@@ -99,6 +104,8 @@ def tile_timeception_pa_t_kernel(tc, x, w, b, dw, bn, out):
         make_identity(nc, ident_f32[:])
         ident_bf16 = const.tile([P, P], BF16, name="ident_bf16")
         make_identity(nc, ident_bf16[:])
+        minus_half = const.tile([P, NV, G], F32, name="minus_half")
+        nc.gpsimd.memset(minus_half[:], -0.5)
 
         w_codes = keep.tile([P, NV, 4, P], U32, name="w_codes", align_bytes=64)
         w_scales = keep.tile([P, NV, 4, P], U8, name="w_scales", align_bytes=64)
@@ -113,9 +120,7 @@ def tile_timeception_pa_t_kernel(tc, x, w, b, dw, bn, out):
             stage = w_stage[n]
             dst = stage[:, 1, :].rearrange("q (m o t) -> q m o t", m=4, t=4)
             src = stage[:, 0, :].rearrange("q (m t o) -> q m o t", m=4, t=4)
-            if engine == "scalar":
-                nc.scalar.copy(out=dst, in_=src)
-            elif engine == "vector":
+            if engine == "vector":
                 nc.vector.tensor_copy(out=dst, in_=src)
             else:
                 nc.gpsimd.tensor_scalar(out=dst, in0=src, scalar1=1.0, scalar2=0.0, op0=ALU.mult, op1=ALU.add)
@@ -156,15 +161,19 @@ def tile_timeception_pa_t_kernel(tc, x, w, b, dw, bn, out):
             src = x_banks[(s, j)][:].rearrange("p h u r -> p h r u")
             nc.scalar.copy(out=dst, in_=src)
 
-        def quant_x(s, g):
-            codes = x_mx.tile([P, 2 * PASS_COLS], U32, name="codes", align_bytes=64)
-            scales = x_mx.tile([P, 2 * PASS_COLS], U8, name="scales", align_bytes=64)
-            nc.vector.quantize_mx(
-                out=codes[:].bitcast(FP8X4),
-                scales=scales[:],
-                in_=x_regrouped[(s, g)][:].rearrange("p a c -> p (a c)"),
-            )
-            x_quantised[(s, g)] = (codes, scales)
+        def quant_x(s, g, pieces=None):
+            if (s, g) not in x_quantised:
+                codes = x_mx.tile([P, 2 * PASS_COLS], U32, name="codes", align_bytes=64)
+                scales = x_mx.tile([P, 2 * PASS_COLS], U8, name="scales", align_bytes=64)
+                x_quantised[(s, g)] = (codes, scales)
+            codes, scales = x_quantised[(s, g)]
+            values = x_regrouped[(s, g)][:].rearrange("p a c -> p (a c)")
+            for c, nl in pieces or [(0, 0)]:
+                lo = c * PASS_COLS + nl * SEG
+                hi = lo + SEG if pieces else 2 * PASS_COLS
+                nc.vector.quantize_mx(
+                    out=codes[:, lo:hi].bitcast(FP8X4), scales=scales[:, lo:hi], in_=values[:, 4 * lo:4 * hi],
+                )
 
         y_banks = {}
         best0 = {}
@@ -210,13 +219,13 @@ def tile_timeception_pa_t_kernel(tc, x, w, b, dw, bn, out):
                     func=ACT.Identity, scale=taps_scaled[:, i, 0, g:g + 1], bias=constant[:, i, g:g + 1],
                 )
 
-        def start_acc():
-            for i in reversed(range(3)):
-                for g in range(G):
-                    nc.gpsimd.tensor_scalar(
-                        out=acc[:, 2 * i + g, :, 0:(i + 1) * HW], in0=zeros[:, :, 0:(i + 1) * HW],
-                        scalar1=zeros[:, 0, 0:1], scalar2=const_start[:, i, g:g + 1], op0=ALU.mult, op1=ALU.add,
-                    )
+        def start_acc(v):
+            i = v - 1
+            for g in range(G):
+                nc.gpsimd.tensor_scalar(
+                    out=acc[:, 2 * i + g, :, 0:v * HW], in0=zeros[:, :, 0:v * HW],
+                    scalar1=zeros[:, 0, 0:1], scalar2=const_start[:, i, g:g + 1], op0=ALU.mult, op1=ALU.add,
+                )
 
         def first_read(s, v):
             t0 = (s % NCH) * NH
@@ -259,11 +268,12 @@ def tile_timeception_pa_t_kernel(tc, x, w, b, dw, bn, out):
                 first = t0 if tcn == 0 else t0 - 1
                 end = t0 + NH
                 neighbours = short.tile([P, G, 2, (NH + 1) * HW], F32, name="neighbours")
-                nc.vector.tensor_tensor(
-                    out=neighbours[:, :, :, (first - t0 + 1) * HW:(end - t0 + 1) * HW].rearrange("p g n c -> p (g n) c"),
-                    in0=even4[:, :, :, first * HW:end * HW].rearrange("p g n c -> p (g n) c"),
-                    in1=even4[:, :, :, (first + 1) * HW:(end + 1) * HW].rearrange("p g n c -> p (g n) c"), op=ALU.max,
-                )
+                for g in range(G):
+                    nc.vector.tensor_tensor(
+                        out=neighbours[:, g, :, (first - t0 + 1) * HW:(end - t0 + 1) * HW],
+                        in0=even4[:, g, :, first * HW:end * HW], in1=even4[:, g, :, (first + 1) * HW:(end + 1) * HW],
+                        op=ALU.max,
+                    )
                 best4[s] = short.tile([P, G, 2, NH * HW], F32, name="best4")
                 for g in range(G):
                     nc.vector.scalar_tensor_tensor(
@@ -308,12 +318,23 @@ def tile_timeception_pa_t_kernel(tc, x, w, b, dw, bn, out):
                     )
                 return
             pairs = acc_pairs[:, 4 * (v - 1):4 * v, t0:t0 + NH]
-            nc.vector.tensor_tensor(
-                out=pooled[s][:, 2 * v:2 * v + 2, :].rearrange("p g (n t q) -> p (g n) t q", n=2, q=HW),
-                in0=pairs[:, :, :, 0, :], in1=pairs[:, :, :, 1, :], op=ALU.max,
-            )
+            dst = pooled[s][:, 2 * v:2 * v + 2, :].rearrange("p g (n t q) -> p (g n) t q", n=2, q=HW)
+            if (s, v) == LAST_POOLED:
+                for nl in range(2):
+                    nc.vector.tensor_tensor(
+                        out=dst[:, nl::2], in0=pairs[:, nl::2, :, 0, :], in1=pairs[:, nl::2, :, 1, :], op=ALU.max,
+                    )
+                return
+            nc.vector.tensor_tensor(out=dst, in0=pairs[:, :, :, 0, :], in1=pairs[:, :, :, 1, :], op=ALU.max)
 
         def transpose_back(s, v):
+            if (s, v) == LAST_POOLED:
+                for nl in range(2):
+                    bank = ps_y.tile([P, 2, P], F32, name="back_last", tag="y")
+                    for g in range(G):
+                        nc.tensor.transpose(bank[:, g, :], pooled[s][:, 2 * v + g, nl * P:(nl + 1) * P], ident_f32[:])
+                    back_banks[(s, v, nl)] = bank
+                return
             bank = ps_back.tile([P, 2, 2, P], F32, name="back", tag="back")
             for nl in range(2):
                 for g in range(G):
@@ -323,6 +344,18 @@ def tile_timeception_pa_t_kernel(tc, x, w, b, dw, bn, out):
         def relu_and_store(s, v):
             pair, tcn = divmod(s, NCH)
             by_branch = s >= STORE_BY_BRANCH_FROM
+            rows = [out[2 * pair + nl, tcn * NH:(tcn + 1) * NH].rearrange("t p q c -> (t p q) c") for nl in range(2)]
+            if (s, v) == LAST_POOLED:
+                for nl in range(2):
+                    last = out_last.tile([P, OUT_V], F32, name="last")
+                    dst = last[:].rearrange("p (o g) -> p o g", g=2)
+                    values = back_banks[(s, v, nl)][:].rearrange("p g o -> p o g")
+                    if nl == 0:
+                        nc.scalar.activation(out=dst, in_=values, func=ACT.Relu)
+                    else:
+                        nc.vector.tensor_scalar_max(out=dst, in0=values, scalar1=0.0)
+                    nc.sync.dma_start(out=rows[nl][:, v * OUT_V:(v + 1) * OUT_V], in_=last[:])
+                return
             if by_branch:
                 small = out_small.tile([P, 2, OUT_V], F32, name="small")
                 dst = small[:]
@@ -335,7 +368,6 @@ def tile_timeception_pa_t_kernel(tc, x, w, b, dw, bn, out):
                 out=dst.rearrange("p n (o g) -> p n o g", g=2),
                 in_=back_banks[(s, v)][:].rearrange("p n g o -> p n o g"), func=ACT.Relu,
             )
-            rows = [out[2 * pair + nl, tcn * NH:(tcn + 1) * NH].rearrange("t p q c -> (t p q) c") for nl in range(2)]
             if by_branch:
                 for nl in range(2):
                     nc.sync.dma_start(out=rows[nl][:, v * OUT_V:(v + 1) * OUT_V], in_=small[:, nl, :])
@@ -373,19 +405,17 @@ def tile_timeception_pa_t_kernel(tc, x, w, b, dw, bn, out):
 
         params_bank = ps_back.tile([P, P], BF16, name="params_bank", tag="back")
         params = const.tile([P, N_PARAM_ROWS], F32, name="params")
-        for nl in range(2):
-            for c in range(2):
-                transpose_x(0, 2 * c + nl, ps_y, "y")
-                copy_out_x(0, 2 * c + nl)
-            if nl == 0:
-                nc.tensor.transpose(params_bank[:], param_rows[:], ident_bf16[:])
-                nc.vector.tensor_copy(out=params[:], in_=params_bank[:, 0:N_PARAM_ROWS])
+        for c in range(2):
+            transpose_x(0, 2 * c, ps_y, "y")
+            copy_out_x(0, 2 * c)
+        nc.tensor.transpose(params_bank[:], param_rows[:], ident_bf16[:])
+        regroup_w(0, "vector")
+        nc.vector.tensor_copy(out=params[:], in_=params_bank[:, 0:N_PARAM_ROWS])
 
         bias = params[:, 0:ROW_DW].rearrange("p (v g) -> p v g", g=2)
         taps = params[:, ROW_DW:ROW_BN].rearrange("p (i j g) -> p i j g", j=3, g=2)
         bn_rows = params[:, ROW_BN:N_PARAM_ROWS].rearrange("p (v k g) -> p v k g", k=4, g=2)
 
-        minus_half = const.tile([P, NV, G], F32, name="minus_half")
         var_eps = const.tile([P, NV, G], F32, name="var_eps")
         rstd = const.tile([P, NV, G], F32, name="rstd")
         work = const.tile([P, NV, G], F32, name="work")
@@ -396,45 +426,54 @@ def tile_timeception_pa_t_kernel(tc, x, w, b, dw, bn, out):
         abs_scale0 = const.tile([P, G], F32, name="abs_scale0")
         taps_scaled = const.tile([P, 3, 3, G], F32, name="taps_scaled")
         tap_bias = const.tile([P, 3, 3, G], F32, name="tap_bias")
-        const_end = const.tile([P, 3, G], F32, name="const_end")
-        const_mid = const.tile([P, 3, G], F32, name="const_mid")
-        const_start = const.tile([P, 3, G], F32, name="const_start")
-        nc.gpsimd.memset(minus_half[:], -0.5)
-        nc.gpsimd.tensor_scalar(
+        tap_sums = const.tile([P, 3, 3, G], F32, name="tap_sums")
+        nc.vector.tensor_scalar(
             out=sign[:], in0=bn_rows[:, :, 0, :], scalar1=0.0, scalar2=2.0, op0=ALU.is_ge, op1=ALU.mult,
         )
-        nc.gpsimd.tensor_scalar_add(out=sign[:], in0=sign[:], scalar1=-1.0)
+        nc.vector.tensor_mul(out=tap_bias[:], in0=taps, in1=bias[:, 1:4, :].unsqueeze(2).to_broadcast([P, 3, 3, G]))
+        nc.vector.tensor_scalar_add(out=sign[:], in0=sign[:], scalar1=-1.0)
+        nc.vector.tensor_add(out=tap_sums[:, 0], in0=tap_bias[:, :, 1, :], in1=tap_bias[:, :, 2, :])
+        nc.vector.tensor_add(out=tap_sums[:, 1], in0=tap_bias[:, :, 0, :], in1=tap_bias[:, :, 1, :])
+        nc.vector.tensor_add(out=tap_sums[:, 2], in0=tap_sums[:, 0], in1=tap_bias[:, :, 0, :])
         nc.gpsimd.tensor_scalar_add(out=var_eps[:], in0=bn_rows[:, :, 3, :], scalar1=EPS)
         nc.gpsimd.tensor_tensor(out=rstd[:], in0=var_eps[:], in1=minus_half[:], op=ALU.pow)
         nc.gpsimd.tensor_mul(out=bn_scale[:], in0=rstd[:], in1=bn_rows[:, :, 0, :])
+        nc.gpsimd.tensor_mul(
+            out=taps_scaled[:], in0=taps, in1=bn_scale[:, 1:4, :].unsqueeze(2).to_broadcast([P, 3, 3, G]),
+        )
         nc.gpsimd.tensor_mul(out=work[:], in0=bn_scale[:], in1=bn_rows[:, :, 2, :])
         nc.gpsimd.tensor_sub(out=bn_shift[:], in0=bn_rows[:, :, 1, :], in1=work[:])
-        def for_each_tap(values):
-            return values[:, 1:4, :].unsqueeze(2).to_broadcast([P, 3, 3, G])
+        nc.gpsimd.tensor_mul(
+            out=tap_sums[:], in0=tap_sums[:], in1=bn_scale[:, 1:4, :].unsqueeze(1).to_broadcast([P, 3, 3, G]),
+        )
+        nc.gpsimd.tensor_add(
+            out=tap_sums[:], in0=tap_sums[:], in1=bn_shift[:, 1:4, :].unsqueeze(1).to_broadcast([P, 3, 3, G]),
+        )
+        const_start, const_end, const_mid = tap_sums[:, 0], tap_sums[:, 1], tap_sums[:, 2]
+        start_acc(3)
 
-        nc.gpsimd.tensor_mul(out=taps_scaled[:], in0=taps, in1=for_each_tap(bn_scale))
-        nc.gpsimd.tensor_mul(out=tap_bias[:], in0=taps_scaled[:], in1=for_each_tap(bias))
-        nc.gpsimd.tensor_add(out=const_start[:], in0=bn_shift[:, 1:4, :], in1=tap_bias[:, :, 1, :])
-        nc.gpsimd.tensor_add(out=const_end[:], in0=const_start[:], in1=tap_bias[:, :, 0, :])
-        nc.gpsimd.tensor_add(out=const_mid[:], in0=const_end[:], in1=tap_bias[:, :, 2, :])
-        nc.gpsimd.tensor_add(out=const_start[:], in0=const_start[:], in1=tap_bias[:, :, 2, :])
-        nc.gpsimd.tensor_mul(out=work[:], in0=bn_scale[:], in1=bias)
-        nc.gpsimd.tensor_add(out=bn_const[:], in0=bn_shift[:], in1=work[:])
-        nc.gpsimd.tensor_mul(out=abs_scale0[:], in0=sign[:, 0, :], in1=bn_scale[:, 0, :])
-        start_acc()
-
-        regroup_w(0, "vector")
-        quant_x(0, 0)
+        quant_x(0, 0, [(0, 0), (1, 0)])
         quant_w(0)
+        for c in range(2):
+            transpose_x(0, 2 * c + 1, ps_y, "y")
+            copy_out_x(0, 2 * c + 1)
+        quant_x(0, 0, [(0, 1), (1, 1)])
+        regroup_w(1, "vector")
+        quant_w(1)
         for nl in range(2):
             for c in range(2):
                 pool, tag = (ps_x, "bank") if nl == 0 else (ps_back, "back")
                 transpose_x(0, 4 + 2 * c + nl, pool, tag)
                 copy_out_x(0, 4 + 2 * c + nl)
-        regroup_w(1, "vector")
-        quant_x(0, 1)
-        regroup_w(2, "scalar")
+            quant_x(0, 1, [(0, nl), (1, nl)])
+        regroup_w(2, "vector")
+        regroup_w(3, "gpsimd")
+        start_acc(2)
         regroup_w(4, "gpsimd")
+        start_acc(1)
+        nc.gpsimd.tensor_mul(out=work[:], in0=bn_scale[:], in1=bias)
+        nc.gpsimd.tensor_add(out=bn_const[:], in0=bn_shift[:], in1=work[:])
+        nc.gpsimd.tensor_mul(out=abs_scale0[:], in0=sign[:, 0, :], in1=bn_scale[:, 0, :])
 
         last_slot = max(back_at)
         for slot in range(last_slot + 1):
@@ -453,12 +492,10 @@ def tile_timeception_pa_t_kernel(tc, x, w, b, dw, bn, out):
                 transpose_back(chunk, branch)
             if has_unit:
                 first_read(s, v)
-            if slot < NV - 1:
+            if 0 < slot < NV - 1:
                 quant_w(slot + 1)
             if has_unit:
                 other_reads(s, v)
-            if slot == 1:
-                regroup_w(3, "vector")
             for chunk, branch in pool_at.get(slot, []):
                 pool_pairs(chunk, branch)
             for n, (c, pair_of_banks) in enumerate(x_pairs):
@@ -472,4 +509,5 @@ def tile_timeception_pa_t_kernel(tc, x, w, b, dw, bn, out):
             for c, g in quant_at.get(slot, []):
                 quant_x(c, g)
             if slot == NV * (NCH - 1):
-                start_acc()
+                for branch in (3, 2, 1):
+                    start_acc(branch)

@@ -27,8 +27,8 @@ OUT_V = G * CB
 ORDER = (4, 3, 2, 1, 0)
 NU = NSTEP * NV
 X_AHEAD = (0, 0, 2, 3, 3, 3, 3, 3)
-POOL_LAG = {0: 0, 1: 1, 2: 1, 3: 1, 4: 0}
-BACK_LAG = 2
+POOL_LAG = {0: 1, 1: 1, 2: 1, 3: 1, 4: 0}
+BACK_LAG = {0: 3, 1: 2, 2: 2, 3: 2, 4: 2}
 STORE_BY_BRANCH_FROM = NSTEP - 2
 LAST_POOLED = (NSTEP - 1, 1)
 ROW_DW = NV * G
@@ -398,10 +398,16 @@ def tile_timeception_pa_t_kernel(tc, x, w, b, dw, bn, out):
         for unit in range(NU):
             s, v = unit // NV, ORDER[unit % NV]
             complete = unit + NV if (s < NSTEP - 1 and v != 0) else unit
+            if unit == NU - 1:
+                put(pool_at, unit, (s, v))
+                put(back_at, unit + 2, (s, v))
+                continue
             put(pool_at, complete + POOL_LAG[v], (s, v))
-            put(back_at, complete + POOL_LAG[v] + BACK_LAG, (s, v))
-        pool_at[NU - 1] = sorted(pool_at[NU - 1])
-        back_at[NU - 1 + BACK_LAG] = sorted(back_at[NU - 1 + BACK_LAG])
+            put(back_at, complete + POOL_LAG[v] + BACK_LAG[v], (s, v))
+        for slot in pool_at:
+            pool_at[slot] = sorted(pool_at[slot], key=lambda e: (e[0], e[1] if slot == NU - 1 else -e[1]))
+        for slot in back_at:
+            back_at[slot] = sorted(back_at[slot])
 
         params_bank = ps_back.tile([P, P], BF16, name="params_bank", tag="back")
         params = const.tile([P, N_PARAM_ROWS], F32, name="params")

@@ -28,7 +28,7 @@ ORDER = (4, 3, 2, 1, 0)
 NU = NSTEP * NV
 X_AHEAD = (0, 0, 2, 3, 3, 3, 3, 3)
 POOL_LAG = {0: 1, 1: 1, 2: 1, 3: 1, 4: 0}
-BACK_LAG = {0: 3, 1: 2, 2: 2, 3: 2, 4: 2}
+BACK_LAG = {0: 3, 1: 3, 2: 2, 3: 2, 4: 2}
 STORE_BY_BRANCH_FROM = NSTEP - 2
 LAST_POOLED = (NSTEP - 1, 1)
 ROW_DW = NV * G
@@ -398,9 +398,9 @@ def tile_timeception_pa_t_kernel(tc, x, w, b, dw, bn, out):
         for unit in range(NU):
             s, v = unit // NV, ORDER[unit % NV]
             complete = unit + NV if (s < NSTEP - 1 and v != 0) else unit
-            if unit == NU - 1:
-                put(pool_at, unit, (s, v))
-                put(back_at, unit + 2, (s, v))
+            if s == NSTEP - 1 and v < 2:
+                put(pool_at, NU - 1, (s, v))
+                put(back_at, NU + 1, (s, v))
                 continue
             put(pool_at, complete + POOL_LAG[v], (s, v))
             put(back_at, complete + POOL_LAG[v] + BACK_LAG[v], (s, v))

@@ -177,6 +177,7 @@ def tile_timeception_pa_t_kernel(tc, x, w, b, dw, bn, out):
 
         y_banks = {}
         best0 = {}
+        pooled = {}
         best4 = {}
 
         def mx_passes(s, v):
@@ -227,6 +228,10 @@ def tile_timeception_pa_t_kernel(tc, x, w, b, dw, bn, out):
                     scalar1=zeros[:, 0, 0:1], scalar2=const_start[:, i, g:g + 1], op0=ALU.mult, op1=ALU.add,
                 )
 
+        def pooled_tile(s):
+            if s not in pooled:
+                pooled[s] = pooled_pool.tile([P, G * NV, SEG], F32, name="pooled", tag="pooled", align_bytes=64)
+
         def first_read(s, v):
             t0 = (s % NCH) * NH
             if v == 0:
@@ -235,7 +240,7 @@ def tile_timeception_pa_t_kernel(tc, x, w, b, dw, bn, out):
                 y = by_parity(y_banks[(s, v, g)])
                 if v == 0:
                     nc.scalar.activation(
-                        out=by_time(best0[s][:, g]), in_=y[:, :, :, 1, :], func=ACT.Copy, scale=sign[:, 0, g:g + 1],
+                        out=by_time(best0[s][:, g]), in_=y[:, :, :, 1, :], func=ACT.Copy, scale=bn_scale[:, 0, g:g + 1],
                     )
                 elif v == 4:
                     nc.scalar.activation(
@@ -258,10 +263,12 @@ def tile_timeception_pa_t_kernel(tc, x, w, b, dw, bn, out):
             tcn = s % NCH
             t0 = tcn * NH
             if v == 0:
+                pooled_tile(s)
                 for g in range(G):
+                    dst = pooled[s][:, g, :].rearrange("p (n c) -> p n c", n=2)
                     nc.vector.scalar_tensor_tensor(
-                        out=by_time(best0[s][:, g]), in0=by_parity(y_banks[(s, v, g)])[:, :, :, 0, :],
-                        scalar=sign[:, 0, g:g + 1], in1=by_time(best0[s][:, g]), op0=ALU.mult, op1=ALU.max,
+                        out=by_time(dst), in0=by_parity(y_banks[(s, v, g)])[:, :, :, 0, :],
+                        scalar=bn_scale[:, 0, g:g + 1], in1=by_time(best0[s][:, g]), op0=ALU.mult, op1=ALU.max,
                     )
                 return
             if v == 4:
@@ -299,22 +306,18 @@ def tile_timeception_pa_t_kernel(tc, x, w, b, dw, bn, out):
                         in1=cells, op0=ALU.mult, op1=ALU.add,
                     )
 
-        pooled = {}
         back_banks = {}
         out_rows = {}
         branches_done = {}
 
         def pool_pairs(s, v):
             t0 = (s % NCH) * NH
-            if s not in pooled:
-                pooled[s] = pooled_pool.tile([P, G * NV, SEG], F32, name="pooled", tag="pooled", align_bytes=64)
-            if v in (0, 4):
-                best, scale = (best0, abs_scale0[:]) if v == 0 else (best4, bn_scale[:, 4, :])
-                engine = nc.vector if (s, v) == (NSTEP - 1, 0) else nc.gpsimd
+            pooled_tile(s)
+            if v == 4:
                 for g in range(G):
-                    engine.tensor_scalar(
-                        out=pooled[s][:, 2 * v + g, :], in0=best[s][:, g].rearrange("p n c -> p (n c)"),
-                        scalar1=scale[:, g:g + 1], scalar2=bn_const[:, v, g:g + 1], op0=ALU.mult, op1=ALU.add,
+                    nc.gpsimd.tensor_scalar(
+                        out=pooled[s][:, 2 * v + g, :], in0=best4[s][:, g].rearrange("p n c -> p (n c)"),
+                        scalar1=bn_scale[:, v, g:g + 1], scalar2=bn_const[:, v, g:g + 1], op0=ALU.mult, op1=ALU.add,
                     )
                 return
             pairs = acc_pairs[:, 4 * (v - 1):4 * v, t0:t0 + NH]
@@ -336,6 +339,17 @@ def tile_timeception_pa_t_kernel(tc, x, w, b, dw, bn, out):
                     back_banks[(s, v, nl)] = bank
                 return
             bank = ps_back.tile([P, 2, 2, P], F32, name="back", tag="back")
+            if v == 0:
+                for nl in range(2):
+                    for g in range(G):
+                        terms = (const0[:, g, :], pooled[s][:, g, nl * P:(nl + 1) * P])
+                        for n, term in enumerate(terms):
+                            nc.tensor.matmul(
+                                bank[:, nl, g, :], lhsT=term, rhs=ident_f32[:], is_transpose=True, start=(n == 0),
+                                stop=(n == 1),
+                            )
+                back_banks[(s, v)] = bank
+                return
             for nl in range(2):
                 for g in range(G):
                     nc.tensor.transpose(bank[:, nl, g, :], pooled[s][:, 2 * v + g, nl * P:(nl + 1) * P], ident_f32[:])
@@ -399,10 +413,12 @@ def tile_timeception_pa_t_kernel(tc, x, w, b, dw, bn, out):
             s, v = unit // NV, ORDER[unit % NV]
             complete = unit + NV if (s < NSTEP - 1 and v != 0) else unit
             if s == NSTEP - 1 and v < 2:
-                put(pool_at, NU - 1, (s, v))
+                if v > 0:
+                    put(pool_at, NU - 1, (s, v))
                 put(back_at, NU + 1, (s, v))
                 continue
-            put(pool_at, complete + POOL_LAG[v], (s, v))
+            if v > 0:
+                put(pool_at, complete + POOL_LAG[v], (s, v))
             put(back_at, complete + POOL_LAG[v] + BACK_LAG[v], (s, v))
         for slot in pool_at:
             pool_at[slot] = sorted(pool_at[slot], key=lambda e: (e[0], e[1] if slot == NU - 1 else -e[1]))
@@ -429,7 +445,7 @@ def tile_timeception_pa_t_kernel(tc, x, w, b, dw, bn, out):
         bn_shift = const.tile([P, NV, G], F32, name="bn_shift")
         bn_const = const.tile([P, NV, G], F32, name="bn_const")
         sign = const.tile([P, NV, G], F32, name="sign")
-        abs_scale0 = const.tile([P, G], F32, name="abs_scale0")
+        const0 = const.tile([P, G, P], F32, name="const0")
         taps_scaled = const.tile([P, 3, 3, G], F32, name="taps_scaled")
         tap_bias = const.tile([P, 3, 3, G], F32, name="tap_bias")
         tap_sums = const.tile([P, 3, 3, G], F32, name="tap_sums")
@@ -479,7 +495,6 @@ def tile_timeception_pa_t_kernel(tc, x, w, b, dw, bn, out):
         start_acc(1)
         nc.gpsimd.tensor_mul(out=work[:], in0=bn_scale[:], in1=bias)
         nc.gpsimd.tensor_add(out=bn_const[:], in0=bn_shift[:], in1=work[:])
-        nc.gpsimd.tensor_mul(out=abs_scale0[:], in0=sign[:, 0, :], in1=bn_scale[:, 0, :])
 
         last_slot = max(back_at)
         for slot in range(last_slot + 1):
@@ -514,6 +529,11 @@ def tile_timeception_pa_t_kernel(tc, x, w, b, dw, bn, out):
                 relu_and_store(chunk, branch)
             for c, g in quant_at.get(slot, []):
                 quant_x(c, g)
+            if slot == NV - 1:
+                for g in range(G):
+                    nc.scalar.activation(
+                        out=const0[:, g, :], in_=ident_f32[:], func=ACT.Identity, scale=0.0, bias=bn_const[:, 0, g:g + 1],
+                    )
             if slot == NV * (NCH - 1):
                 for branch in (3, 2, 1):
                     start_acc(branch)

@@ -30,7 +30,8 @@ X_AHEAD = (0, 0, 2, 3, 3, 3, 3, 3)
 POOL_LAG = {0: 1, 1: 1, 2: 1, 3: 1, 4: 0}
 BACK_LAG = {0: 3, 1: 3, 2: 2, 3: 2, 4: 2}
 STORE_BY_BRANCH_FROM = NSTEP - 2
-LAST_POOLED = (NSTEP - 1, 1)
+LAST_UNITS = ((NSTEP - 1, 0), (NSTEP - 2, 1), (NSTEP - 1, 1))
+LAST_POOLED = LAST_UNITS[2]
 ROW_DW = NV * G
 ROW_BN = ROW_DW + 3 * 3 * G
 N_PARAM_ROWS = ROW_BN + NV * 4 * G
@@ -223,9 +224,9 @@ def tile_timeception_pa_t_kernel(tc, x, w, b, dw, bn, out):
         def start_acc(v):
             i = v - 1
             for g in range(G):
-                nc.gpsimd.tensor_scalar(
-                    out=acc[:, 2 * i + g, :, 0:v * HW], in0=zeros[:, :, 0:v * HW],
-                    scalar1=zeros[:, 0, 0:1], scalar2=const_start[:, i, g:g + 1], op0=ALU.mult, op1=ALU.add,
+                nc.scalar.activation(
+                    out=acc[:, 2 * i + g, :, 0:v * HW], in_=zeros[:, :, 0:v * HW], func=ACT.Identity,
+                    bias=const_start[:, i, g:g + 1],
                 )
 
         def pooled_tile(s):
@@ -338,7 +339,8 @@ def tile_timeception_pa_t_kernel(tc, x, w, b, dw, bn, out):
                         nc.tensor.transpose(bank[:, g, :], pooled[s][:, 2 * v + g, nl * P:(nl + 1) * P], ident_f32[:])
                     back_banks[(s, v, nl)] = bank
                 return
-            bank = ps_back.tile([P, 2, 2, P], F32, name="back", tag="back")
+            pool, tag = (ps_y, "y") if (s, v) in LAST_UNITS else (ps_back, "back")
+            bank = pool.tile([P, 2, 2, P], F32, name="back", tag=tag)
             if v == 0:
                 for nl in range(2):
                     for g in range(G):
@@ -378,10 +380,12 @@ def tile_timeception_pa_t_kernel(tc, x, w, b, dw, bn, out):
                     out_rows[s] = out_pool.tile([P, 2, NV * OUT_V], F32, name="out_rows", tag="out_rows", align_bytes=64)
                     branches_done[s] = 0
                 dst = out_rows[s][:, :, v * OUT_V:(v + 1) * OUT_V]
-            nc.scalar.activation(
-                out=dst.rearrange("p n (o g) -> p n o g", g=2),
-                in_=back_banks[(s, v)][:].rearrange("p n g o -> p n o g"), func=ACT.Relu,
-            )
+            values = back_banks[(s, v)][:].rearrange("p n g o -> p n o g")
+            dst = dst.rearrange("p n (o g) -> p n o g", g=2)
+            if (s, v) == LAST_UNITS[1]:
+                nc.vector.tensor_scalar_max(out=dst, in0=values, scalar1=0.0)
+            else:
+                nc.scalar.activation(out=dst, in_=values, func=ACT.Relu)
             if by_branch:
                 for nl in range(2):
                     nc.sync.dma_start(out=rows[nl][:, v * OUT_V:(v + 1) * OUT_V], in_=small[:, nl, :])
@@ -412,7 +416,7 @@ def tile_timeception_pa_t_kernel(tc, x, w, b, dw, bn, out):
         for unit in range(NU):
             s, v = unit // NV, ORDER[unit % NV]
             complete = unit + NV if (s < NSTEP - 1 and v != 0) else unit
-            if s == NSTEP - 1 and v < 2:
+            if (s, v) in LAST_UNITS:
                 if v > 0:
                     put(pool_at, NU - 1, (s, v))
                 put(back_at, NU + 1, (s, v))
@@ -423,7 +427,7 @@ def tile_timeception_pa_t_kernel(tc, x, w, b, dw, bn, out):
         for slot in pool_at:
             pool_at[slot] = sorted(pool_at[slot], key=lambda e: (e[0], e[1] if slot == NU - 1 else -e[1]))
         for slot in back_at:
-            back_at[slot] = sorted(back_at[slot])
+            back_at[slot] = list(LAST_UNITS) if slot > NU else sorted(back_at[slot])
 
         params_bank = ps_back.tile([P, P], BF16, name="params_bank", tag="back")
         params = const.tile([P, N_PARAM_ROWS], F32, name="params")
@@ -472,7 +476,6 @@ def tile_timeception_pa_t_kernel(tc, x, w, b, dw, bn, out):
             out=tap_sums[:], in0=tap_sums[:], in1=bn_shift[:, 1:4, :].unsqueeze(1).to_broadcast([P, 3, 3, G]),
         )
         const_start, const_end, const_mid = tap_sums[:, 0], tap_sums[:, 1], tap_sums[:, 2]
-        start_acc(3)
 
         quant_x(0, 0, [(0, 0), (1, 0)])
         quant_w(0)
@@ -490,9 +493,7 @@ def tile_timeception_pa_t_kernel(tc, x, w, b, dw, bn, out):
             quant_x(0, 1, [(0, nl), (1, nl)])
         regroup_w(2, "vector")
         regroup_w(3, "gpsimd")
-        start_acc(2)
         regroup_w(4, "gpsimd")
-        start_acc(1)
         nc.gpsimd.tensor_mul(out=work[:], in0=bn_scale[:], in1=bias)
         nc.gpsimd.tensor_add(out=bn_const[:], in0=bn_shift[:], in1=work[:])
 
@@ -513,6 +514,9 @@ def tile_timeception_pa_t_kernel(tc, x, w, b, dw, bn, out):
                 transpose_back(chunk, branch)
             if has_unit:
                 first_read(s, v)
+            if slot in (0, NV * (NCH - 1)):
+                for branch in (3, 2, 1):
+                    start_acc(branch)
             if 0 < slot < NV - 1:
                 quant_w(slot + 1)
             if has_unit:
@@ -534,6 +538,3 @@ def tile_timeception_pa_t_kernel(tc, x, w, b, dw, bn, out):
                     nc.scalar.activation(
                         out=const0[:, g, :], in_=ident_f32[:], func=ACT.Identity, scale=0.0, bias=bn_const[:, 0, g:g + 1],
                     )
-            if slot == NV * (NCH - 1):
-                for branch in (3, 2, 1):
-                    start_acc(branch)

@@ -87,14 +87,14 @@ def tile_timeception_pa_t_kernel(tc, x, w, b, dw, bn, out):
         nc.vector.memset(zeros[:], 0.0)
         spare = const.tile([P, 1], F32, name="spare")
         nc.scalar.copy(out=spare[:], in_=zeros[:, 0, 0:1])
-        load_x(0, 0, [0])
         load_w(0)
+        load_x(0, 0, [0])
+        load_w(1)
         load_x(0, 0, [1])
         nc.sync.dma_start(out=param_rows[ROW_BN:N_PARAM_ROWS, :], in_=bn.rearrange("v k g o -> (v k g) o"))
         nc.sync.dma_start(out=param_rows[ROW_DW:ROW_BN, :], in_=dw.rearrange("i j g o -> (i j g) o"))
         nc.sync.dma_start(out=param_rows[0:ROW_DW, :], in_=b.rearrange("v g o -> (v g) o"))
         load_x(0, 1, [0])
-        load_w(1)
         load_x(0, 1, [1])
         load_w(2)
         load_x(1, 0)
@@ -436,6 +436,8 @@ def tile_timeception_pa_t_kernel(tc, x, w, b, dw, bn, out):
             copy_out_x(0, 2 * c)
         nc.tensor.transpose(params_bank[:], param_rows[:], ident_bf16[:])
         regroup_w(0, "vector")
+        quant_w(0)
+        regroup_w(1, "vector")
         nc.vector.tensor_copy(out=params[:], in_=params_bank[:, 0:N_PARAM_ROWS])
 
         bias = params[:, 0:ROW_DW].rearrange("p (v g) -> p v g", g=2)
@@ -478,12 +480,10 @@ def tile_timeception_pa_t_kernel(tc, x, w, b, dw, bn, out):
         const_start, const_end, const_mid = tap_sums[:, 0], tap_sums[:, 1], tap_sums[:, 2]
 
         quant_x(0, 0, [(0, 0), (1, 0)])
-        quant_w(0)
         for c in range(2):
             transpose_x(0, 2 * c + 1, ps_y, "y")
             copy_out_x(0, 2 * c + 1)
         quant_x(0, 0, [(0, 1), (1, 1)])
-        regroup_w(1, "vector")
         quant_w(1)
         for nl in range(2):
             for c in range(2):

from contextlib import ExitStack

import concourse.mybir as mybir
from concourse.masks import make_identity

F32 = mybir.dt.float32
BF16 = mybir.dt.bfloat16
U32 = mybir.dt.uint32
U8 = mybir.dt.uint8
FP8X4 = mybir.dt.float8_e4m3fn_x4
ALU = mybir.AluOpType
ACT = mybir.ActivationFunctionType

P = 128
B, T, HW, G, K, CB, NV = 4, 64, 16, 2, 1024, 128, 5
EPS = 1e-3
FLOPS = 2 * B * T * HW * G * K * NV * CB

TC = 16
NCH = T // TC
SEG = TC * HW
NH = TC // 2
NSTEP = (B // 2) * NCH
PASS_COLS = 2 * SEG
OUT_V = G * CB

ORDER = (4, 3, 2, 1, 0)
NU = NSTEP * NV
X_AHEAD = (0, 0, 2, 3, 3, 3, 3, 3)
POOL_LAG = {0: 1, 1: 1, 2: 1, 3: 1, 4: 0}
BACK_LAG = {0: 3, 1: 3, 2: 2, 3: 2, 4: 2}
STORE_BY_BRANCH_FROM = NSTEP - 2
LAST_UNITS = ((NSTEP - 1, 0), (NSTEP - 2, 1), (NSTEP - 1, 1))
LAST_POOLED = LAST_UNITS[2]
ROW_DW = NV * G
ROW_BN = ROW_DW + 3 * 3 * G
N_PARAM_ROWS = ROW_BN + NV * 4 * G
PASS_WORDS = 256


def tile_timeception_pa_t_kernel(tc, x, w, b, dw, bn, out):
    nc = tc.nc
    with ExitStack() as ctx:
        ctx.enter_context(tc.manual_schedule())
        const = ctx.enter_context(tc.tile_pool(name="const", bufs=1))
        keep = ctx.enter_context(tc.tile_pool(name="keep", bufs=1))
        x_in = ctx.enter_context(tc.tile_pool(name="x_in", bufs=4))
        x_grouped = ctx.enter_context(tc.tile_pool(name="x_grouped", bufs=2))
        x_mx = ctx.enter_context(tc.tile_pool(name="x_mx", bufs=4))
        short = ctx.enter_context(tc.tile_pool(name="short", bufs=2))
        out_small = ctx.enter_context(tc.tile_pool(name="out_small", bufs=2 * NV - 1))
        out_last = ctx.enter_context(tc.tile_pool(name="out_last", bufs=2))
        pooled_pool = ctx.enter_context(tc.tile_pool(name="pooled_pool", bufs=2))
        out_pool = ctx.enter_context(tc.tile_pool(name="out_pool", bufs=2))
        ps_x = ctx.enter_context(tc.psum_pool(name="ps_x", bufs=2))
        ps_y = ctx.enter_context(tc.psum_pool(name="ps_y", bufs=4))
        ps_back = ctx.enter_context(tc.psum_pool(name="ps_back", bufs=2))

        x_raw = {}

        def load_x(s, g, batches=(0, 1)):
            pair, tcn = divmod(s, NCH)
            if (s, g) not in x_raw:
                x_raw[(s, g)] = x_in.tile([P, 4, K], BF16, name="raw")
            raw = x_raw[(s, g)]
            for nl in batches:
                src = x[2 * pair + nl, tcn * TC:(tcn + 1) * TC]
                nc.sync.dma_start(
                    out=raw[:, 2 * nl:2 * nl + 2, :],
                    in_=src.rearrange("(h t) p q c -> (t p q) h c", h=2)[:, :, g * K:(g + 1) * K],
                )

        w_stage = {}

        def load_w(n):
            pool, tag = (pooled_pool, "pooled") if n % 2 == 0 else (out_pool, "out_rows")
            stage = pool.tile([P, 2, 16 * P], BF16, name="stage", tag=tag, align_bytes=64)
            nc.sync.dma_start(
                out=stage[:, 0, :].rearrange("q (a f) -> q a f", f=4 * P),
                in_=w[ORDER[n]].rearrange("g (a q t) o -> q (g a) (t o)", q=P, t=4),
            )
            w_stage[n] = stage

        param_rows = const.tile([P, P], BF16, name="param_rows")
        nc.vector.memset(param_rows[:], 0.0)
        zeros = const.tile([P, 2, 3 * HW], F32, name="zeros")
        nc.vector.memset(zeros[:], 0.0)
        spare = const.tile([P, 1], F32, name="spare")
        nc.scalar.copy(out=spare[:], in_=zeros[:, 0, 0:1])
        load_w(0)
        load_x(0, 0, [0])
        load_w(1)
        load_x(0, 0, [1])
        nc.sync.dma_start(out=param_rows[ROW_BN:N_PARAM_ROWS, :], in_=bn.rearrange("v k g o -> (v k g) o"))
        nc.sync.dma_start(out=param_rows[ROW_DW:ROW_BN, :], in_=dw.rearrange("i j g o -> (i j g) o"))
        nc.sync.dma_start(out=param_rows[0:ROW_DW, :], in_=b.rearrange("v g o -> (v g) o"))
        load_x(0, 1, [0])
        load_x(0, 1, [1])
        load_w(2)
        load_x(1, 0)
        load_w(3)
        load_x(1, 1)
        load_w(4)
        ident_f32 = const.tile([P, P], F32, name="ident_f32")
        make_identity(nc, ident_f32[:])
        ident_bf16 = const.tile([P, P], BF16, name="ident_bf16")
        make_identity(nc, ident_bf16[:])
        minus_half = const.tile([P, NV, G], F32, name="minus_half")
        nc.gpsimd.memset(minus_half[:], -0.5)

        w_codes = keep.tile([P, NV, 4, P], U32, name="w_codes", align_bytes=64)
        w_scales = keep.tile([P, NV, 4, P], U8, name="w_scales", align_bytes=64)
        acc = keep.tile([P, 6, 2, T * HW], F32, name="acc")
        even4 = keep.tile([P, G, 2, (T // 2 + 1) * HW], F32, name="even4")
        early_cells = even4[:, :, :, 0:T // 2 * HW].rearrange("p g n (k c) -> p (g n) k c", k=NCH)[:, :, 1:, 0:HW]
        nc.gpsimd.memset(early_cells, 0.0)
        last4 = keep.tile([P, 2, G, 2, HW], F32, name="last4")
        acc_pairs = acc[:].rearrange("p k n (t r q) -> p (k n) t r q", r=2, q=HW)

        def regroup_w(n, engine):
            stage = w_stage[n]
            dst = stage[:, 1, :].rearrange("q (m o t) -> q m o t", m=4, t=4)
            src = stage[:, 0, :].rearrange("q (m t o) -> q m o t", m=4, t=4)
            if engine == "vector":
                nc.vector.tensor_copy(out=dst, in_=src)
            else:
                nc.gpsimd.tensor_scalar(out=dst, in0=src, scalar1=1.0, scalar2=0.0, op0=ALU.mult, op1=ALU.add)

        def quant_w(n):
            v = ORDER[n]
            nc.vector.quantize_mx(
                out=w_codes[:, v].rearrange("q m o -> q (m o)").bitcast(FP8X4),
                scales=w_scales[:, v].rearrange("q m o -> q (m o)"),
                in_=w_stage[n][:, 1, :],
            )

        x_regrouped = {}
        x_banks = {}
        x_quantised = {}

        def bank_of(j):
            return j // 4, (j // 2) % 2, j % 2

        def transpose_x(s, j, pool=ps_x, tag="bank"):
            g, c, nl = bank_of(j)
            words = x_raw[(s, g)][:].bitcast(F32)
            bank = pool.tile([P, 2, 2, P], F32, name="bank", tag=tag)
            for h in range(2):
                for u in range(2):
                    lo = c * PASS_WORDS
                    nc.tensor.transpose(
                        bank[:, h, u, :], words[:, 2 * nl + h, lo + u:lo + PASS_WORDS:2], ident_f32[:],
                    )
            x_banks[(s, j)] = bank

        def copy_out_x(s, j):
            g, c, nl = bank_of(j)
            if (s, g) not in x_regrouped:
                x_regrouped[(s, g)] = x_grouped.tile([P, 2, 4 * PASS_COLS], BF16, name="grouped", align_bytes=64)
            words = x_regrouped[(s, g)][:].bitcast(F32)
            dst = words[:, c, nl * 2 * SEG:(nl + 1) * 2 * SEG].rearrange("p (h r u) -> p h r u", h=2, u=2)
            src = x_banks[(s, j)][:].rearrange("p h u r -> p h r u")
            nc.scalar.copy(out=dst, in_=src)

        def quant_x(s, g, pieces=None):
            if (s, g) not in x_quantised:
                codes = x_mx.tile([P, 2 * PASS_COLS], U32, name="codes", align_bytes=64)
                scales = x_mx.tile([P, 2 * PASS_COLS], U8, name="scales", align_bytes=64)
                x_quantised[(s, g)] = (codes, scales)
            codes, scales = x_quantised[(s, g)]
            values = x_regrouped[(s, g)][:].rearrange("p a c -> p (a c)")
            for c, nl in pieces or [(0, 0)]:
                lo = c * PASS_COLS + nl * SEG
                hi = lo + SEG if pieces else 2 * PASS_COLS
                nc.vector.quantize_mx(
                    out=codes[:, lo:hi].bitcast(FP8X4), scales=scales[:, lo:hi], in_=values[:, 4 * lo:4 * hi],
                )

        y_banks = {}
        best0 = {}
        pooled = {}
        best4 = {}

        def mx_passes(s, v):
            for g in range(G):
                codes, scales = x_quantised[(s, g)]
                y = ps_y.tile([P, PASS_COLS], F32, name="y")
                for c in range(2):
                    nc.tensor.matmul_mx(
                        out=y[:],
                        lhsT=w_codes[:, v, 2 * g + c, :].bitcast(FP8X4),
                        lhsT_scale=w_scales[:, v, 2 * g + c, :],
                        rhs=codes[:, c * PASS_COLS:(c + 1) * PASS_COLS].bitcast(FP8X4),
                        rhs_scale=scales[:, c * PASS_COLS:(c + 1) * PASS_COLS],
                        start=(c == 0),
                        stop=(c == 1),
                    )
                y_banks[(s, v, g)] = y

        def by_batch(y):
            return y[:].rearrange("p (n c) -> p n c", n=2)

        def by_parity(y):
            return y[:].rearrange("p (n t r q) -> p n t r q", n=2, r=2, q=HW)

        def by_time(cells):
            return cells.rearrange("p n (t q) -> p n t q", q=HW)

        def first_tap(s, v, g):
            tcn = s % NCH
            i = v - 1
            shift = HW * v
            if tcn < NCH - 1:
                pieces = [(0, SEG, const_mid)]
            else:
                pieces = [(0, SEG - 2 * shift, const_mid), (SEG - 2 * shift, SEG - shift, const_end)]
            for lo, hi, constant in pieces:
                at = tcn * SEG + shift
                nc.scalar.activation(
                    out=acc[:, 2 * i + g, :, at + lo:at + hi], in_=by_batch(y_banks[(s, v, g)])[:, :, lo:hi],
                    func=ACT.Identity, scale=taps_scaled[:, i, 0, g:g + 1], bias=constant[:, i, g:g + 1],
                )

        def start_acc(v):
            i = v - 1
            for g in range(G):
                nc.scalar.activation(
                    out=acc[:, 2 * i + g, :, 0:v * HW], in_=zeros[:, :, 0:v * HW], func=ACT.Identity,
                    bias=const_start[:, i, g:g + 1],
                )

        def pooled_tile(s):
            if s not in pooled:
                pooled[s] = pooled_pool.tile([P, G * NV, SEG], F32, name="pooled", tag="pooled", align_bytes=64)

        def first_read(s, v):
            t0 = (s % NCH) * NH
            if v == 0:
                best0[s] = short.tile([P, G, 2, NH * HW], F32, name="best0")
            for g in range(G):
                y = by_parity(y_banks[(s, v, g)])
                if v == 0:
                    nc.scalar.activation(
                        out=by_time(best0[s][:, g]), in_=y[:, :, :, 1, :], func=ACT.Copy, scale=bn_scale[:, 0, g:g + 1],
                    )
                elif v == 4:
                    nc.scalar.activation(
                        out=by_time(even4[:, g, :, t0 * HW:(t0 + NH) * HW]), in_=y[:, :, :, 0, :], func=ACT.Copy,
                        scale=sign[:, 4, g:g + 1],
                    )
                else:
                    first_tap(s, v, g)
            if v == 4:
                for g in range(G):
                    y_last = by_parity(y_banks[(s, v, g)])[:, :, NH - 1, 1, :]
                    if s % NCH < NCH - 1:
                        nc.scalar.copy(out=last4[:, s % 2, g], in_=y_last)
                    else:
                        nc.scalar.activation(
                            out=even4[:, g, :, T // 2 * HW:], in_=y_last, func=ACT.Copy, scale=sign[:, 4, g:g + 1],
                        )

        def other_reads(s, v):
            tcn = s % NCH
            t0 = tcn * NH
            if v == 0:
                pooled_tile(s)
                for g in range(G):
                    dst = pooled[s][:, g, :].rearrange("p (n c) -> p n c", n=2)
                    nc.vector.scalar_tensor_tensor(
                        out=by_time(dst), in0=by_parity(y_banks[(s, v, g)])[:, :, :, 0, :],
                        scalar=bn_scale[:, 0, g:g + 1], in1=by_time(best0[s][:, g]), op0=ALU.mult, op1=ALU.max,
                    )
                return
            if v == 4:
                first = t0 if tcn == 0 else t0 - 1
                end = t0 + NH
                neighbours = short.tile([P, G, 2, (NH + 1) * HW], F32, name="neighbours")
                for g in range(G):
                    nc.vector.tensor_tensor(
                        out=neighbours[:, g, :, (first - t0 + 1) * HW:(end - t0 + 1) * HW],
                        in0=even4[:, g, :, first * HW:end * HW], in1=even4[:, g, :, (first + 1) * HW:(end + 1) * HW],
                        op=ALU.max,
                    )
                best4[s] = short.tile([P, G, 2, NH * HW], F32, name="best4")
                for g in range(G):
                    nc.vector.scalar_tensor_tensor(
                        out=by_time(best4[s][:, g]), in0=by_time(neighbours[:, g, :, HW:]), scalar=sign[:, 4, g:g + 1],
                        in1=by_parity(y_banks[(s, v, g)])[:, :, :, 1, :], op0=ALU.mult, op1=ALU.max,
                    )
                if tcn > 0:
                    for g in range(G):
                        nc.vector.scalar_tensor_tensor(
                            out=best4[s - 1][:, g, :, (NH - 1) * HW:], in0=neighbours[:, g, :, 0:HW],
                            scalar=sign[:, 4, g:g + 1], in1=last4[:, (s - 1) % 2, g], op0=ALU.mult, op1=ALU.max,
                        )
                return
            i = v - 1
            shift = HW * v
            skip = shift if tcn == 0 else 0
            for j, lo in ((1, 0), (2, skip)):
                at = tcn * SEG - (j - 1) * shift
                for g in range(G):
                    cells = acc[:, 2 * i + g, :, at + lo:at + SEG]
                    nc.vector.scalar_tensor_tensor(
                        out=cells, in0=by_batch(y_banks[(s, v, g)])[:, :, lo:SEG], scalar=taps_scaled[:, i, j, g:g + 1],
                        in1=cells, op0=ALU.mult, op1=ALU.add,
                    )

        back_banks = {}
        out_rows = {}
        branches_done = {}

        def pool_pairs(s, v):
            t0 = (s % NCH) * NH
            pooled_tile(s)
            if v == 4:
                for g in range(G):
                    nc.gpsimd.tensor_scalar(
                        out=pooled[s][:, 2 * v + g, :], in0=best4[s][:, g].rearrange("p n c -> p (n c)"),
                        scalar1=bn_scale[:, v, g:g + 1], scalar2=bn_const[:, v, g:g + 1], op0=ALU.mult, op1=ALU.add,
                    )
                return
            pairs = acc_pairs[:, 4 * (v - 1):4 * v, t0:t0 + NH]
            dst = pooled[s][:, 2 * v:2 * v + 2, :].rearrange("p g (n t q) -> p (g n) t q", n=2, q=HW)
            if (s, v) == LAST_POOLED:
                for nl in range(2):
                    nc.vector.tensor_tensor(
                        out=dst[:, nl::2], in0=pairs[:, nl::2, :, 0, :], in1=pairs[:, nl::2, :, 1, :], op=ALU.max,
                    )
                return
            nc.vector.tensor_tensor(out=dst, in0=pairs[:, :, :, 0, :], in1=pairs[:, :, :, 1, :], op=ALU.max)

        def transpose_back(s, v):
            if (s, v) == LAST_POOLED:
                for nl in range(2):
                    bank = ps_y.tile([P, 2, P], F32, name="back_last", tag="y")
                    for g in range(G):
                        nc.tensor.transpose(bank[:, g, :], pooled[s][:, 2 * v + g, nl * P:(nl + 1) * P], ident_f32[:])
                    back_banks[(s, v, nl)] = bank
                return
            pool, tag = (ps_y, "y") if (s, v) in LAST_UNITS else (ps_back, "back")
            bank = pool.tile([P, 2, 2, P], F32, name="back", tag=tag)
            if v == 0:
                for nl in range(2):
                    for g in range(G):
                        terms = (const0[:, g, :], pooled[s][:, g, nl * P:(nl + 1) * P])
                        for n, term in enumerate(terms):
                            nc.tensor.matmul(
                                bank[:, nl, g, :], lhsT=term, rhs=ident_f32[:], is_transpose=True, start=(n == 0),
                                stop=(n == 1),
                            )
                back_banks[(s, v)] = bank
                return
            for nl in range(2):
                for g in range(G):
                    nc.tensor.transpose(bank[:, nl, g, :], pooled[s][:, 2 * v + g, nl * P:(nl + 1) * P], ident_f32[:])
            back_banks[(s, v)] = bank

        def relu_and_store(s, v):
            pair, tcn = divmod(s, NCH)
            by_branch = s >= STORE_BY_BRANCH_FROM
            rows = [out[2 * pair + nl, tcn * NH:(tcn + 1) * NH].rearrange("t p q c -> (t p q) c") for nl in range(2)]
            if (s, v) == LAST_POOLED:
                for nl in range(2):
                    last = out_last.tile([P, OUT_V], F32, name="last")
                    dst = last[:].rearrange("p (o g) -> p o g", g=2)
                    values = back_banks[(s, v, nl)][:].rearrange("p g o -> p o g")
                    if nl == 0:
                        nc.scalar.activation(out=dst, in_=values, func=ACT.Relu)
                    else:
                        nc.vector.tensor_scalar_max(out=dst, in0=values, scalar1=0.0)
                    nc.sync.dma_start(out=rows[nl][:, v * OUT_V:(v + 1) * OUT_V], in_=last[:])
                return
            if by_branch:
                small = out_small.tile([P, 2, OUT_V], F32, name="small")
                dst = small[:]
            else:
                if s not in out_rows:
                    out_rows[s] = out_pool.tile([P, 2, NV * OUT_V], F32, name="out_rows", tag="out_rows", align_bytes=64)
                    branches_done[s] = 0
                dst = out_rows[s][:, :, v * OUT_V:(v + 1) * OUT_V]
            values = back_banks[(s, v)][:].rearrange("p n g o -> p n o g")
            dst = dst.rearrange("p n (o g) -> p n o g", g=2)
            if (s, v) == LAST_UNITS[1]:
                nc.vector.tensor_scalar_max(out=dst, in0=values, scalar1=0.0)
            else:
                nc.scalar.activation(out=dst, in_=values, func=ACT.Relu)
            if by_branch:
                for nl in range(2):
                    nc.sync.dma_start(out=rows[nl][:, v * OUT_V:(v + 1) * OUT_V], in_=small[:, nl, :])
                return
            branches_done[s] = branches_done[s] + 1
            if branches_done[s] == NV:
                for nl in range(2):
                    nc.sync.dma_start(out=rows[nl], in_=out_rows[s][:, nl, :])

        def put(table, slot, item):
            table[slot] = table.get(slot, []) + [item]

        x_stage_at = {}
        quant_at = {}
        load_at = {}
        pool_at = {}
        back_at = {}
        x_stage_end = {0: -1}
        for c in range(1, NSTEP):
            first = NV * (c - 1) - X_AHEAD[c]
            for pair_of_banks in range(4):
                put(x_stage_at, first + pair_of_banks, (c, pair_of_banks))
            put(quant_at, first + 2, (c, 0))
            put(quant_at, first + 3, (c, 1))
            x_stage_end[c] = first + 3
        for c in range(2, NSTEP):
            put(load_at, max(0, x_stage_end[c - 2] + 1), c)
        for unit in range(NU):
            s, v = unit // NV, ORDER[unit % NV]
            complete = unit + NV if (s < NSTEP - 1 and v != 0) else unit
            if (s, v) in LAST_UNITS:
                if v > 0:
                    put(pool_at, NU - 1, (s, v))
                put(back_at, NU + 1, (s, v))
                continue
            if v > 0:
                put(pool_at, complete + POOL_LAG[v], (s, v))
            put(back_at, complete + POOL_LAG[v] + BACK_LAG[v], (s, v))
        for slot in pool_at:
            pool_at[slot] = sorted(pool_at[slot], key=lambda e: (e[0], e[1] if slot == NU - 1 else -e[1]))
        for slot in back_at:
            back_at[slot] = list(LAST_UNITS) if slot > NU else sorted(back_at[slot])

        params_bank = ps_back.tile([P, P], BF16, name="params_bank", tag="back")
        params = const.tile([P, N_PARAM_ROWS], F32, name="params")
        for c in range(2):
            transpose_x(0, 2 * c, ps_y, "y")
            copy_out_x(0, 2 * c)
        nc.tensor.transpose(params_bank[:], param_rows[:], ident_bf16[:])
        regroup_w(0, "vector")
        quant_w(0)
        regroup_w(1, "vector")
        nc.vector.tensor_copy(out=params[:], in_=params_bank[:, 0:N_PARAM_ROWS])

        bias = params[:, 0:ROW_DW].rearrange("p (v g) -> p v g", g=2)
        taps = params[:, ROW_DW:ROW_BN].rearrange("p (i j g) -> p i j g", j=3, g=2)
        bn_rows = params[:, ROW_BN:N_PARAM_ROWS].rearrange("p (v k g) -> p v k g", k=4, g=2)

        var_eps = const.tile([P, NV, G], F32, name="var_eps")
        rstd = const.tile([P, NV, G], F32, name="rstd")
        work = const.tile([P, NV, G], F32, name="work")
        bn_scale = const.tile([P, NV, G], F32, name="bn_scale")
        bn_shift = const.tile([P, NV, G], F32, name="bn_shift")
        bn_const = const.tile([P, NV, G], F32, name="bn_const")
        sign = const.tile([P, NV, G], F32, name="sign")
        const0 = const.tile([P, G, P], F32, name="const0")
        taps_scaled = const.tile([P, 3, 3, G], F32, name="taps_scaled")
        tap_bias = const.tile([P, 3, 3, G], F32, name="tap_bias")
        tap_sums = const.tile([P, 3, 3, G], F32, name="tap_sums")
        nc.vector.tensor_scalar(
            out=sign[:], in0=bn_rows[:, :, 0, :], scalar1=0.0, scalar2=2.0, op0=ALU.is_ge, op1=ALU.mult,
        )
        nc.vector.tensor_mul(out=tap_bias[:], in0=taps, in1=bias[:, 1:4, :].unsqueeze(2).to_broadcast([P, 3, 3, G]))
        nc.vector.tensor_scalar_add(out=sign[:], in0=sign[:], scalar1=-1.0)
        nc.vector.tensor_add(out=tap_sums[:, 0], in0=tap_bias[:, :, 1, :], in1=tap_bias[:, :, 2, :])
        nc.vector.tensor_add(out=tap_sums[:, 1], in0=tap_bias[:, :, 0, :], in1=tap_bias[:, :, 1, :])
        nc.vector.tensor_add(out=tap_sums[:, 2], in0=tap_sums[:, 0], in1=tap_bias[:, :, 0, :])
        nc.gpsimd.tensor_scalar_add(out=var_eps[:], in0=bn_rows[:, :, 3, :], scalar1=EPS)
        nc.gpsimd.tensor_tensor(out=rstd[:], in0=var_eps[:], in1=minus_half[:], op=ALU.pow)
        nc.gpsimd.tensor_mul(out=bn_scale[:], in0=rstd[:], in1=bn_rows[:, :, 0, :])
        nc.gpsimd.tensor_mul(
            out=taps_scaled[:], in0=taps, in1=bn_scale[:, 1:4, :].unsqueeze(2).to_broadcast([P, 3, 3, G]),
        )
        nc.gpsimd.tensor_mul(out=work[:], in0=bn_scale[:], in1=bn_rows[:, :, 2, :])
        nc.gpsimd.tensor_sub(out=bn_shift[:], in0=bn_rows[:, :, 1, :], in1=work[:])
        nc.gpsimd.tensor_mul(
            out=tap_sums[:], in0=tap_sums[:], in1=bn_scale[:, 1:4, :].unsqueeze(1).to_broadcast([P, 3, 3, G]),
        )
        nc.gpsimd.tensor_add(
            out=tap_sums[:], in0=tap_sums[:], in1=bn_shift[:, 1:4, :].unsqueeze(1).to_broadcast([P, 3, 3, G]),
        )
        const_start, const_end, const_mid = tap_sums[:, 0], tap_sums[:, 1], tap_sums[:, 2]

        quant_x(0, 0, [(0, 0), (1, 0)])
        for c in range(2):
            transpose_x(0, 2 * c + 1, ps_y, "y")
            copy_out_x(0, 2 * c + 1)
        quant_x(0, 0, [(0, 1), (1, 1)])
        quant_w(1)
        for nl in range(2):
            for c in range(2):
                pool, tag = (ps_x, "bank") if nl == 0 else (ps_back, "back")
                transpose_x(0, 4 + 2 * c + nl, pool, tag)
                copy_out_x(0, 4 + 2 * c + nl)
            quant_x(0, 1, [(0, nl), (1, nl)])
        regroup_w(2, "vector")
        regroup_w(3, "gpsimd")
        regroup_w(4, "gpsimd")
        nc.gpsimd.tensor_mul(out=work[:], in0=bn_scale[:], in1=bias)
        nc.gpsimd.tensor_add(out=bn_const[:], in0=bn_shift[:], in1=work[:])

        last_slot = max(back_at)
        for slot in range(last_slot + 1):
            s, v = slot // NV, ORDER[slot % NV]
            has_unit = slot < NU
            x_pairs = x_stage_at.get(slot, [])
            for c in load_at.get(slot, []):
                for g in range(G):
                    load_x(c, g)
            if has_unit:
                mx_passes(s, v)
            for c, pair_of_banks in x_pairs[:1]:
                transpose_x(c, 2 * pair_of_banks)
                transpose_x(c, 2 * pair_of_banks + 1)
            for chunk, branch in back_at.get(slot, []):
                transpose_back(chunk, branch)
            if has_unit:
                first_read(s, v)
            if slot in (0, NV * (NCH - 1)):
                for branch in (3, 2, 1):
                    start_acc(branch)
            if 0 < slot < NV - 1:
                quant_w(slot + 1)
            if has_unit:
                other_reads(s, v)
            for chunk, branch in pool_at.get(slot, []):
                pool_pairs(chunk, branch)
            for n, (c, pair_of_banks) in enumerate(x_pairs):
                if n > 0:
                    transpose_x(c, 2 * pair_of_banks)
                    transpose_x(c, 2 * pair_of_banks + 1)
                copy_out_x(c, 2 * pair_of_banks)
                copy_out_x(c, 2 * pair_of_banks + 1)
            for chunk, branch in back_at.get(slot, []):
                relu_and_store(chunk, branch)
            for c, g in quant_at.get(slot, []):
                quant_x(c, g)
            if slot == NV - 1:
                for g in range(G):
                    nc.scalar.activation(
                        out=const0[:, g, :], in_=ident_f32[:], func=ACT.Identity, scale=0.0, bias=bn_const[:, 0, g:g + 1],
                    )
